import numpy as np
import ml_dtypes


def mxq(x, axis, fmt="e4m3"):
    dtype, down = {"e4m3": (ml_dtypes.float8_e4m3fn, 7), "e5m2": (ml_dtypes.float8_e5m2, 14)}[fmt]
    v = np.moveaxis(np.asarray(x, np.float32).astype(ml_dtypes.bfloat16).astype(np.float64), axis, -1)
    blocks = v.reshape(v.shape[:-1] + (-1, 32))
    amax = np.abs(blocks).max(-1, keepdims=True)
    byte = np.maximum(np.where(amax > 0, np.frexp(amax)[1] - 1 + 127, 0) - down, 1)
    scale = np.exp2(byte - 127.0)
    codes = (blocks / scale).astype(np.float32).astype(dtype).astype(np.float64)
    return np.moveaxis((codes * scale).reshape(v.shape), -1, axis)


WIDE = False


def mx_kscale(k, group=512):
    if not WIDE:
        return np.ones(k)
    levels = np.array([18, -18])
    if group != 512:
        return np.exp2(np.random.permutation(np.resize(levels, k // group))).repeat(group)
    if k % 512:
        return np.exp2(np.random.permutation(np.resize(levels, k // 32))).repeat(32)
    a = np.empty((k // 512, 16))
    for p in range(k // 512):
        a[p, :8] = np.random.permutation(np.resize(levels, 8))
        for g in range(8):
            far = levels[np.abs(levels - a[p, g]) >= 10]
            a[p, g + 8] = far[np.random.randint(len(far))]
    return np.exp2(a.ravel()).repeat(32)


BF16 = ml_dtypes.bfloat16


def bf(x):
    return np.asarray(x, np.float32).astype(BF16)


def f64(x):
    return np.asarray(x).astype(np.float64)


B, N, VD, QD, D, H, NG, P = 32, 32, 2048, 1024, 1024, 2, 20, 64
DH = D // H
T = B * N


def preact(out_t, out_w, out_b, self_feat):
    t = f64(out_t).reshape(T, H, D).swapaxes(0, 1)
    nb = t @ f64(out_w)
    return f64(self_feat) + nb.swapaxes(0, 1).reshape(B, N, D) + f64(out_b)


def setup_inputs():
    s = mx_kscale(T).reshape(B, N, 1)
    u = mx_kscale(D, group=128)
    t0 = bf(np.random.standard_normal((B, N, H, D)) * 0.7)
    w0 = bf(np.random.standard_normal((H, D, DH)) / np.sqrt(D))
    out_b = bf(np.random.standard_normal(D) * 0.3)
    self_feat = bf(np.random.standard_normal((B, N, D)) * 0.9)
    vis = bf(np.maximum(np.random.standard_normal((B, N, D)), 0.0))
    g = bf(4.0 * np.random.standard_normal((B, N, D)) * np.exp2(np.random.randint(-6, 1, (B, N, 1))) / s * u)
    z = preact(t0, w0, out_b, self_feat)
    return {"out_t": bf(f64(t0) * s[..., None]),
            "out_w": bf(f64(w0) / u.reshape(H, 1, DH)),
            "out_b": out_b,
            "self_feat": self_feat,
            "vis": vis,
            "z": np.asarray(z, np.float32),
            "grad_out": g}


def reference(out_t, out_w, out_b, self_feat, vis, z, grad_out):
    dz = np.where(f64(z) > 0.0, f64(grad_out), 0.0)
    dz = dz.reshape(T, H, DH).swapaxes(0, 1)
    x = f64(out_t).reshape(T, H, D).swapaxes(0, 1)
    dt = mxq(dz, 2, "e5m2") @ mxq(f64(out_w), 2, "e4m3").swapaxes(1, 2)
    dw = mxq(x, 1, "e4m3").swapaxes(1, 2) @ mxq(dz, 1, "e5m2")
    return dt.swapaxes(0, 1).reshape(B, N, H, D), dw

@@ -1,0 +1,297 @@
+from contextlib import ExitStack
+
+import concourse.mybir as mybir
+from concourse.masks import make_identity
+
+T, H, D, DH = 1024, 2, 1024, 512
+FLOPS = 4 * T * H * D * DH
+BYTES = 2 * T * H * D + 2 * H * D * DH + 4 * T * H * DH + 2 * T * H * DH + 4 * T * H * D + 4 * H * D * DH
+
+P = 128
+PACK = 4
+GROUP = P * PACK
+W = 1
+E = 4 // W
+GROUPS = T // GROUP
+CHUNK = 512
+
+F32 = mybir.dt.float32
+BF16 = mybir.dt.bfloat16
+U32 = mybir.dt.uint32
+U8 = mybir.dt.uint8
+E4X4 = mybir.dt.float8_e4m3fn_x4
+E5X4 = mybir.dt.float8_e5m2_x4
+GT = mybir.AluOpType.is_gt
+MULT = mybir.AluOpType.mult
+
+
+def tile_implicitrelationencoder_pb_v_kernel(
+    tc, out_t, out_w, out_b, self_feat, vis, z, grad_out, out_0, out_1
+):
+    nc = tc.nc
+    x_rows = out_t.rearrange("b n h d -> (b n) (h d)")
+    z_rows = z.rearrange("b n d -> (b n) d")
+    g_rows = grad_out.rearrange("b n d -> (b n) d")
+    o0_rows = out_0.rearrange("b n h d -> (b n) (h d)")
+
+    def group_view(rows, g):
+        return rows[g * GROUP : (g + 1) * GROUP, :].rearrange("(p j) d -> p j d", j=PACK)
+
+    with ExitStack() as ctx:
+        keep = ctx.enter_context(tc.tile_pool(name="keep", bufs=1))
+        work = ctx.enter_context(tc.tile_pool(name="work", bufs=1))
+        psum = ctx.enter_context(tc.psum_pool(name="psum", bufs=1))
+
+        ident = keep.tile([P, P], F32, name="ident")
+        make_identity(nc, ident[:])
+
+        xq = keep.tile([P, GROUPS * H * 2, CHUNK], U32, name="xq", align_bytes=64)
+        xs = keep.tile([P, GROUPS * H * 2, CHUNK], U8, name="xs", align_bytes=64)
+        tq = keep.tile([P, GROUPS * H, CHUNK], U32, name="tq", align_bytes=64)
+        ts = keep.tile([P, GROUPS * H, CHUNK], U8, name="ts", align_bytes=64)
+        fq = keep.tile([P, GROUPS * H, CHUNK], U32, name="fq", align_bytes=64)
+        fs = keep.tile([P, GROUPS * H, CHUNK], U8, name="fs", align_bytes=64)
+        wq = keep.tile([P, H * 2, CHUNK], U32, name="wq", align_bytes=64)
+        ws = keep.tile([P, H * 2, CHUNK], U8, name="ws", align_bytes=64)
+
+        z_sb, g_sb, w_sb, x_sb, dz_sb = {}, {}, {}, {}, {}
+
+        def open_group(g):
+            z_sb[g] = work.tile([P, PACK, H * DH], F32, name="zt", tag="k16", bufs=4)
+            g_sb[g] = work.tile([P, PACK, H * DH], BF16, name="gt", tag="g8", bufs=2)
+            dz_sb[g] = work.tile([P, PACK, H * DH], BF16, name="dzt", tag="dz", bufs=2, align_bytes=64)
+
+        def load_dz_rows(g, lo, hi):
+            js = slice(lo, hi)
+            nc.sync.dma_start(out=z_sb[g][:, js, :], in_=group_view(z_rows, g)[:, js, :])
+            nc.sync.dma_start(out=g_sb[g][:, js, :], in_=group_view(g_rows, g)[:, js, :])
+
+        def load_w(h, c):
+            if c == 0:
+                w_sb[h] = work.tile([P, 2, 4 * DH], BF16, name="wt", tag="w8", bufs=2)
+            nc.sync.dma_start(
+                out=w_sb[h][:, c, :], in_=out_w[h].rearrange("(c q m) o -> c q (m o)", c=2, m=4)[c]
+            )
+
+        def load_x(g):
+            x_sb[g] = work.tile([P, PACK, H * D], BF16, name="xt", tag="x16", bufs=2)
+            nc.sync.dma_start(out=x_sb[g][:], in_=group_view(x_rows, g))
+
+        def make_dz(g, lo, hi):
+            js = slice(lo, hi)
+            nc.vector.scalar_tensor_tensor(
+                out=dz_sb[g][:, js, :], in0=z_sb[g][:, js, :], scalar=0.0,
+                in1=g_sb[g][:, js, :], op0=GT, op1=MULT,
+            )
+
+        def copy_on(engine, out, in_):
+            if engine == "v":
+                nc.vector.tensor_copy(out=out, in_=in_)
+            else:
+                nc.scalar.copy(out=out, in_=in_)
+
+        fgrp = {}
+
+        def turn_dz(g, a, engines):
+            grp = work.tile([P, 2048], BF16, name="fgrp", tag="grp", bufs=4, align_bytes=64)
+            fgrp[g, a] = grp
+            words = dz_sb[g][:].rearrange("p j w -> p (j w)").bitcast(F32)
+            for h in range(H):
+                tp = psum.tile([P, 4, P], F32, name="tp", tag="tp", bufs=3)
+                for jj in range(2):
+                    for u in range(2):
+                        off = (2 * a + jj) * 512 + h * 256
+                        nc.tensor.transpose(tp[:, 2 * jj + u, :], words[:, off + u : off + 256 : 2], ident[:])
+                copy_on(
+                    engines[h],
+                    out=grp[:].bitcast(F32)[:, h * 512 : (h + 1) * 512].rearrange("p (j r u) -> p j r u", j=2, u=2),
+                    in_=tp[:].rearrange("p (j u) r -> p j r u", u=2),
+                )
+
+        def quant_dz_feat(g, a, h):
+            cols = slice(a * 256, (a + 1) * 256)
+            nc.vector.quantize_mx(
+                out=fq[:, g * H + h, cols].bitcast(E5X4), scales=fs[:, g * H + h, cols],
+                in_=fgrp[g, a][:, h * 1024 : (h + 1) * 1024],
+            )
+
+        wgrp = {}
+
+        def turn_w(h, c, engines):
+            grp = work.tile([P, 2048], BF16, name="wgrp", tag="grp", bufs=4, align_bytes=64)
+            wgrp[h, c] = grp
+            words = w_sb[h][:].rearrange("p c r -> p (c r)").bitcast(F32)
+            dst = grp[:].bitcast(F32).rearrange("p (q k) -> p q k", k=8)
+            for mm in range(2):
+                tp = psum.tile([P, 4, P], F32, name="tp", tag="tp", bufs=3)
+                for i in range(2):
+                    for u in range(2):
+                        off = c * 1024 + (2 * mm + i) * 256
+                        nc.tensor.transpose(tp[:, 2 * i + u, :], words[:, off + u : off + 256 : 2], ident[:])
+                copy_on(engines[mm], out=dst[:, :, 4 * mm : 4 * mm + 4], in_=tp[:].rearrange("p k q -> p q k"))
+
+        def quant_w(h, c):
+            nc.vector.quantize_mx(out=wq[:, 2 * h + c, :].bitcast(E4X4), scales=ws[:, 2 * h + c, :], in_=wgrp[h, c][:])
+
+        tgrp = {}
+
+        def lay_dz_tok(g, h, engine):
+            grp = work.tile([P, 2048], BF16, name="tgrp", tag="il", bufs=4, align_bytes=64)
+            tgrp[g, h] = grp
+            copy_on(
+                engine,
+                out=grp[:].rearrange("p (c i j) -> p c j i", i=4, j=PACK),
+                in_=dz_sb[g][:, :, h * DH : (h + 1) * DH].rearrange("p j (c i) -> p c j i", i=4),
+            )
+
+        def quant_dz_tok(g, h):
+            nc.vector.quantize_mx(out=tq[:, g * H + h, :].bitcast(E5X4), scales=ts[:, g * H + h, :], in_=tgrp[g, h][:])
+
+        xgrp = {}
+
+        def lay_x(g, i, engine):
+            grp = work.tile([P, 2048], BF16, name="xgrp", tag="il", bufs=4, align_bytes=64)
+            xgrp[g, i] = grp
+            copy_on(
+                engine,
+                out=grp[:].rearrange("p (c i j) -> p c j i", i=4, j=PACK),
+                in_=x_sb[g][:, :, i * CHUNK : (i + 1) * CHUNK].rearrange("p j (c i) -> p c j i", i=4),
+            )
+
+        def quant_x(g, i):
+            nc.vector.quantize_mx(out=xq[:, g * 4 + i, :].bitcast(E4X4), scales=xs[:, g * 4 + i, :], in_=xgrp[g, i][:])
+
+        o0_sb = {}
+
+        pending = []
+
+        def flush():
+            for dst, src in pending:
+                nc.scalar.dma_start(out=dst, in_=src)
+            pending.clear()
+
+        def make_out0(g, j, engines="ssss"):
+            if j % 2 == 0:
+                o0_sb[g] = work.tile([P, 2, H * D], F32, name="o0", tag="k16", bufs=4)
+            rows = slice(j * P, (j + 1) * P)
+            for h in range(H):
+                for c in range(2):
+                    acc = psum.tile([P, CHUNK], F32, name="acc", tag="acc", bufs=5)
+                    nc.tensor.matmul_mx(
+                        out=acc[:],
+                        lhsT=fq[:, g * H + h, rows].bitcast(E5X4), lhsT_scale=fs[:, g * H + h, rows],
+                        rhs=wq[:, 2 * h + c, :].bitcast(E4X4), rhs_scale=ws[:, 2 * h + c, :],
+                        start=True, stop=True,
+                    )
+                    copy_on(
+                        engines[2 * h + c],
+                        out=o0_sb[g][:, j % 2, (2 * h + c) * CHUNK : (2 * h + c + 1) * CHUNK], in_=acc[:],
+                    )
+                    if h == 0 and c == 1:
+                        flush()
+            if j % 2 == 0:
+                nc.sync.dma_start(out=group_view(o0_rows, g)[:, j, :], in_=o0_sb[g][:, j % 2, :])
+            else:
+                pending.append((group_view(o0_rows, g)[:, j, :], o0_sb[g][:, j % 2, :]))
+
+        o1_sb = {}
+
+        def make_out1(h, c, engines):
+            if c == 0:
+                o1_sb[h] = work.tile([P, 2, E, W * DH], F32, name="o1", tag="x16", bufs=2)
+            for i in range(4):
+                cols = slice(i * P, (i + 1) * P)
+                m, e = divmod(i, E)
+                acc = psum.tile([P, CHUNK], F32, name="acc", tag="acc", bufs=5)
+                for g in range(GROUPS):
+                    nc.tensor.matmul_mx(
+                        out=acc[:],
+                        lhsT=xq[:, g * 4 + 2 * h + c, cols].bitcast(E4X4), lhsT_scale=xs[:, g * 4 + 2 * h + c, cols],
+                        rhs=tq[:, g * H + h, :].bitcast(E5X4), rhs_scale=ts[:, g * H + h, :],
+                        start=(g == 0), stop=(g == GROUPS - 1),
+                    )
+                copy_on(engines[i], out=o1_sb[h][:, c, e, m * DH : (m + 1) * DH], in_=acc[:])
+                if i == 1:
+                    flush()
+            view = out_1[h].rearrange("(c e q m) o -> c q e (m o)", c=2, e=E, m=W)[c]
+            if (h, c) == (1, 1):
+                nc.sync.dma_start(out=view[:, 0:2, :], in_=o1_sb[h][:, c, 0:2, :])
+                nc.scalar.dma_start(out=view[:, 2:4, :], in_=o1_sb[h][:, c, 2:4, :])
+            elif c == 0:
+                nc.sync.dma_start(out=view, in_=o1_sb[h][:, c, :, :])
+            else:
+                pending.append((view, o1_sb[h][:, c, :, :]))
+
+        with tc.manual_schedule():
+            open_group(0)
+            open_group(1)
+            load_dz_rows(0, 0, 2)
+            load_dz_rows(0, 2, 4)
+            load_w(0, 0)
+            load_w(0, 1)
+            load_dz_rows(1, 0, 2)
+            load_w(1, 0)
+            load_w(1, 1)
+            load_dz_rows(1, 2, 4)
+            load_x(0)
+            load_x(1)
+            make_dz(0, 0, 2)
+            turn_dz(0, 0, "ss")
+            make_dz(0, 2, 4)
+            turn_dz(0, 1, "ss")
+            lay_dz_tok(0, 0, "v")
+            quant_dz_feat(0, 0, 0)
+            quant_dz_feat(0, 0, 1)
+            lay_dz_tok(0, 1, "v")
+            quant_dz_tok(0, 0)
+            quant_dz_feat(0, 1, 0)
+            quant_dz_feat(0, 1, 1)
+            turn_w(0, 0, "ss")
+            turn_w(0, 1, "ss")
+            quant_w(0, 0)
+            make_dz(1, 0, 2)
+            quant_w(0, 1)
+            quant_dz_tok(0, 1)
+            turn_w(1, 0, "ss")
+            turn_w(1, 1, "ss")
+            quant_w(1, 0)
+            quant_w(1, 1)
+            turn_dz(1, 0, "ss")
+            make_dz(1, 2, 4)
+            make_out0(0, 0, "ssss")
+            make_out0(0, 1, "ssss")
+            turn_dz(1, 1, "ss")
+            lay_dz_tok(1, 0, "v")
+            quant_dz_feat(1, 0, 0)
+            quant_dz_feat(1, 0, 1)
+            make_out0(0, 2, "ssss")
+            lay_dz_tok(1, 1, "v")
+            quant_dz_tok(1, 0)
+            quant_dz_feat(1, 1, 0)
+            quant_dz_feat(1, 1, 1)
+            make_out0(0, 3, "ssss")
+            lay_x(0, 0, "v")
+            quant_dz_tok(1, 1)
+            make_out0(1, 0, "ssss")
+            lay_x(0, 1, "v")
+            quant_x(0, 0)
+            make_out0(1, 1, "ssss")
+            lay_x(0, 2, "v")
+            quant_x(0, 1)
+            make_out0(1, 2, "ssss")
+            lay_x(0, 3, "v")
+            quant_x(0, 2)
+            make_out0(1, 3, "ssss")
+            lay_x(1, 0, "v")
+            quant_x(0, 3)
+            lay_x(1, 1, "v")
+            quant_x(1, 0)
+            make_out1(0, 0, "ssss")
+            lay_x(1, 2, "v")
+            quant_x(1, 1)
+            make_out1(0, 1, "ssss")
+            lay_x(1, 3, "v")
+            quant_x(1, 2)
+            make_out1(1, 0, "ssss")
+            quant_x(1, 3)
+            make_out1(1, 1, "svsv")

@@ -10,10 +10,9 @@ BYTES = 2 * T * H * D + 2 * H * D * DH + 4 * T * H * DH + 2 * T * H * DH + 4 * T
 P = 128
 PACK = 4
 GROUP = P * PACK
-W = 1
-E = 4 // W
 GROUPS = T // GROUP
 CHUNK = 512
+W_ROWS = D // P
 
 F32 = mybir.dt.float32
 BF16 = mybir.dt.bfloat16
@@ -49,40 +48,40 @@ def tile_implicitrelationencoder_pb_v_kernel(
         xs = keep.tile([P, GROUPS * H * 2, CHUNK], U8, name="xs", align_bytes=64)
         tq = keep.tile([P, GROUPS * H, CHUNK], U32, name="tq", align_bytes=64)
         ts = keep.tile([P, GROUPS * H, CHUNK], U8, name="ts", align_bytes=64)
-        fq = keep.tile([P, GROUPS * H, CHUNK], U32, name="fq", align_bytes=64)
-        fs = keep.tile([P, GROUPS * H, CHUNK], U8, name="fs", align_bytes=64)
+        fq = keep.tile([P, GROUPS * 2, CHUNK], U32, name="fq", align_bytes=64)
+        fs = keep.tile([P, GROUPS * 2, CHUNK], U8, name="fs", align_bytes=64)
         wq = keep.tile([P, H * 2, CHUNK], U32, name="wq", align_bytes=64)
         ws = keep.tile([P, H * 2, CHUNK], U8, name="ws", align_bytes=64)
 
-        z_sb, g_sb, w_sb, x_sb, dz_sb = {}, {}, {}, {}, {}
+        z_sb, g_sb, w_sb, x_sb = {}, {}, {}, {}
 
         def open_group(g):
-            z_sb[g] = work.tile([P, PACK, H * DH], F32, name="zt", tag="k16", bufs=4)
-            g_sb[g] = work.tile([P, PACK, H * DH], BF16, name="gt", tag="g8", bufs=2)
-            dz_sb[g] = work.tile([P, PACK, H * DH], BF16, name="dzt", tag="dz", bufs=2, align_bytes=64)
+            z_sb[g] = work.tile([P, PACK, H * DH], F32, name="zt", tag="k16", bufs=6)
+            g_sb[g] = work.tile([P, PACK, H * DH], BF16, name="gt", tag="k8", bufs=4)
 
         def load_dz_rows(g, lo, hi):
             js = slice(lo, hi)
             nc.sync.dma_start(out=z_sb[g][:, js, :], in_=group_view(z_rows, g)[:, js, :])
             nc.sync.dma_start(out=g_sb[g][:, js, :], in_=group_view(g_rows, g)[:, js, :])
 
-        def load_w(h, c):
-            if c == 0:
-                w_sb[h] = work.tile([P, 2, 4 * DH], BF16, name="wt", tag="w8", bufs=2)
-            nc.sync.dma_start(
-                out=w_sb[h][:, c, :], in_=out_w[h].rearrange("(c q m) o -> c q (m o)", c=2, m=4)[c]
-            )
+        def load_w(h):
+            w_sb[h] = work.tile([P, W_ROWS * DH], BF16, name="wt", tag="k8", bufs=4)
+            nc.sync.dma_start(out=w_sb[h][:], in_=out_w[h].rearrange("(q m) o -> q (m o)", m=W_ROWS))
 
         def load_x(g):
-            x_sb[g] = work.tile([P, PACK, H * D], BF16, name="xt", tag="x16", bufs=2)
+            x_sb[g] = work.tile([P, PACK, H * D], BF16, name="xt", tag="k16", bufs=6)
             nc.sync.dma_start(out=x_sb[g][:], in_=group_view(x_rows, g))
 
-        def make_dz(g, lo, hi):
-            js = slice(lo, hi)
-            nc.vector.scalar_tensor_tensor(
-                out=dz_sb[g][:, js, :], in0=z_sb[g][:, js, :], scalar=0.0,
-                in1=g_sb[g][:, js, :], op0=GT, op1=MULT,
-            )
+        def make_dz(g, a):
+            js = slice(2 * a, 2 * a + 2)
+            for u in range(2):
+                nc.vector.scalar_tensor_tensor(
+                    out=dz_all[g][:, js, :].rearrange("p j (h u w e) -> p u j h w e", h=H, u=2, e=2)[:, u],
+                    in0=z_sb[g][:, js, :].rearrange("p j (h w u e) -> p u j h w e", h=H, u=2, e=2)[:, u],
+                    scalar=0.0,
+                    in1=g_sb[g][:, js, :].rearrange("p j (h w u e) -> p u j h w e", h=H, u=2, e=2)[:, u],
+                    op0=GT, op1=MULT,
+                )
 
         def copy_on(engine, out, in_):
             if engine == "v":
@@ -90,58 +89,60 @@ def tile_implicitrelationencoder_pb_v_kernel(
             else:
                 nc.scalar.copy(out=out, in_=in_)
 
+        dz_all = {}
+        for g in range(GROUPS):
+            dz_all[g] = keep.tile([P, PACK, H * DH], BF16, name="dz%d" % g, align_bytes=64)
+
         fgrp = {}
 
-        def turn_dz(g, a, engines):
-            grp = work.tile([P, 2048], BF16, name="fgrp", tag="grp", bufs=4, align_bytes=64)
+        def turn_dz(g, a):
+            grp = work.tile([P, 2048], BF16, name="fgrp", tag="grp", bufs=3, align_bytes=64)
             fgrp[g, a] = grp
-            words = dz_sb[g][:].rearrange("p j w -> p (j w)").bitcast(F32)
+            words = dz_all[g][:].rearrange("p j w -> p (j w)").bitcast(F32)
             for h in range(H):
                 tp = psum.tile([P, 4, P], F32, name="tp", tag="tp", bufs=3)
                 for jj in range(2):
                     for u in range(2):
-                        off = (2 * a + jj) * 512 + h * 256
-                        nc.tensor.transpose(tp[:, 2 * jj + u, :], words[:, off + u : off + 256 : 2], ident[:])
-                copy_on(
-                    engines[h],
+                        off = (2 * a + jj) * 512 + h * 256 + u * P
+                        nc.tensor.transpose(tp[:, 2 * jj + u, :], words[:, off : off + P], ident[:])
+                nc.scalar.copy(
                     out=grp[:].bitcast(F32)[:, h * 512 : (h + 1) * 512].rearrange("p (j r u) -> p j r u", j=2, u=2),
                     in_=tp[:].rearrange("p (j u) r -> p j r u", u=2),
                 )
 
-        def quant_dz_feat(g, a, h):
-            cols = slice(a * 256, (a + 1) * 256)
-            nc.vector.quantize_mx(
-                out=fq[:, g * H + h, cols].bitcast(E5X4), scales=fs[:, g * H + h, cols],
-                in_=fgrp[g, a][:, h * 1024 : (h + 1) * 1024],
-            )
+        def quant_dz_feat(g, a):
+            nc.vector.quantize_mx(out=fq[:, 2 * g + a, :].bitcast(E5X4), scales=fs[:, 2 * g + a, :], in_=fgrp[g, a][:])
 
         wgrp = {}
 
-        def turn_w(h, c, engines):
-            grp = work.tile([P, 2048], BF16, name="wgrp", tag="grp", bufs=4, align_bytes=64)
-            wgrp[h, c] = grp
-            words = w_sb[h][:].rearrange("p c r -> p (c r)").bitcast(F32)
-            dst = grp[:].bitcast(F32).rearrange("p (q k) -> p q k", k=8)
-            for mm in range(2):
+        def turn_w(h):
+            grp = work.tile([P, 4096], BF16, name="wgrp", tag="wgrp", bufs=2, align_bytes=64)
+            wgrp[h] = grp
+            words = w_sb[h][:].bitcast(F32)
+            dst = grp[:].bitcast(F32).rearrange("p (q k) -> p q k", k=2 * W_ROWS)
+            for mm in range(W_ROWS // 2):
                 tp = psum.tile([P, 4, P], F32, name="tp", tag="tp", bufs=3)
                 for i in range(2):
                     for u in range(2):
-                        off = c * 1024 + (2 * mm + i) * 256
+                        off = (2 * mm + i) * 256
                         nc.tensor.transpose(tp[:, 2 * i + u, :], words[:, off + u : off + 256 : 2], ident[:])
-                copy_on(engines[mm], out=dst[:, :, 4 * mm : 4 * mm + 4], in_=tp[:].rearrange("p k q -> p q k"))
+                nc.scalar.copy(out=dst[:, :, 4 * mm : 4 * mm + 4], in_=tp[:].rearrange("p k q -> p q k"))
 
-        def quant_w(h, c):
-            nc.vector.quantize_mx(out=wq[:, 2 * h + c, :].bitcast(E4X4), scales=ws[:, 2 * h + c, :], in_=wgrp[h, c][:])
+        def quant_w(h):
+            nc.vector.quantize_mx(
+                out=wq[:, 2 * h : 2 * h + 2, :].rearrange("p c n -> p (c n)").bitcast(E4X4),
+                scales=ws[:, 2 * h : 2 * h + 2, :].rearrange("p c n -> p (c n)"),
+                in_=wgrp[h][:],
+            )
 
         tgrp = {}
 
-        def lay_dz_tok(g, h, engine):
-            grp = work.tile([P, 2048], BF16, name="tgrp", tag="il", bufs=4, align_bytes=64)
+        def lay_dz_tok(g, h):
+            grp = work.tile([P, 2048], BF16, name="tgrp", tag="il", bufs=3, align_bytes=64)
             tgrp[g, h] = grp
-            copy_on(
-                engine,
+            nc.vector.tensor_copy(
                 out=grp[:].rearrange("p (c i j) -> p c j i", i=4, j=PACK),
-                in_=dz_sb[g][:, :, h * DH : (h + 1) * DH].rearrange("p j (c i) -> p c j i", i=4),
+                in_=dz_all[g][:, :, h * DH : (h + 1) * DH].rearrange("p j (c i) -> p c j i", i=4),
             )
 
         def quant_dz_tok(g, h):
@@ -149,11 +150,10 @@ def tile_implicitrelationencoder_pb_v_kernel(
 
         xgrp = {}
 
-        def lay_x(g, i, engine):
-            grp = work.tile([P, 2048], BF16, name="xgrp", tag="il", bufs=4, align_bytes=64)
+        def lay_x(g, i):
+            grp = work.tile([P, 2048], BF16, name="xgrp", tag="il", bufs=3, align_bytes=64)
             xgrp[g, i] = grp
-            copy_on(
-                engine,
+            nc.vector.tensor_copy(
                 out=grp[:].rearrange("p (c i j) -> p c j i", i=4, j=PACK),
                 in_=x_sb[g][:, :, i * CHUNK : (i + 1) * CHUNK].rearrange("p j (c i) -> p c j i", i=4),
             )
@@ -163,135 +163,94 @@ def tile_implicitrelationencoder_pb_v_kernel(
 
         o0_sb = {}
 
-        pending = []
-
-        def flush():
-            for dst, src in pending:
-                nc.scalar.dma_start(out=dst, in_=src)
-            pending.clear()
-
-        def make_out0(g, j, engines="ssss"):
-            if j % 2 == 0:
-                o0_sb[g] = work.tile([P, 2, H * D], F32, name="o0", tag="k16", bufs=4)
-            rows = slice(j * P, (j + 1) * P)
-            for h in range(H):
+        def make_out0(g, a, h):
+            if h == 0:
+                o0_sb[g, a] = work.tile([P, 2, H * D], F32, name="o0", tag="k16", bufs=6)
+            for jj in range(2):
+                rows = slice(h * 256 + jj * P, h * 256 + (jj + 1) * P)
                 for c in range(2):
                     acc = psum.tile([P, CHUNK], F32, name="acc", tag="acc", bufs=5)
                     nc.tensor.matmul_mx(
                         out=acc[:],
-                        lhsT=fq[:, g * H + h, rows].bitcast(E5X4), lhsT_scale=fs[:, g * H + h, rows],
+                        lhsT=fq[:, 2 * g + a, rows].bitcast(E5X4), lhsT_scale=fs[:, 2 * g + a, rows],
                         rhs=wq[:, 2 * h + c, :].bitcast(E4X4), rhs_scale=ws[:, 2 * h + c, :],
                         start=True, stop=True,
                     )
-                    copy_on(
-                        engines[2 * h + c],
-                        out=o0_sb[g][:, j % 2, (2 * h + c) * CHUNK : (2 * h + c + 1) * CHUNK], in_=acc[:],
-                    )
-                    if h == 0 and c == 1:
-                        flush()
-            if j % 2 == 0:
-                nc.sync.dma_start(out=group_view(o0_rows, g)[:, j, :], in_=o0_sb[g][:, j % 2, :])
-            else:
-                pending.append((group_view(o0_rows, g)[:, j, :], o0_sb[g][:, j % 2, :]))
+                    nc.scalar.copy(out=o0_sb[g, a][:, jj, (2 * h + c) * CHUNK : (2 * h + c + 1) * CHUNK], in_=acc[:])
+            if h == H - 1:
+                nc.sync.dma_start(out=group_view(o0_rows, g)[:, 2 * a : 2 * a + 2, :], in_=o0_sb[g, a][:])
 
-        o1_sb = {}
-
-        def make_out1(h, c, engines):
-            if c == 0:
-                o1_sb[h] = work.tile([P, 2, E, W * DH], F32, name="o1", tag="x16", bufs=2)
-            for i in range(4):
-                cols = slice(i * P, (i + 1) * P)
-                m, e = divmod(i, E)
+        def make_out1(i, engines):
+            h, c = divmod(i, 2)
+            o1 = work.tile([P, 4, DH], F32, name="o1", tag="k8", bufs=4)
+            for e in range(4):
+                cols = slice(e * P, (e + 1) * P)
                 acc = psum.tile([P, CHUNK], F32, name="acc", tag="acc", bufs=5)
                 for g in range(GROUPS):
                     nc.tensor.matmul_mx(
                         out=acc[:],
-                        lhsT=xq[:, g * 4 + 2 * h + c, cols].bitcast(E4X4), lhsT_scale=xs[:, g * 4 + 2 * h + c, cols],
+                        lhsT=xq[:, g * 4 + i, cols].bitcast(E4X4), lhsT_scale=xs[:, g * 4 + i, cols],
                         rhs=tq[:, g * H + h, :].bitcast(E5X4), rhs_scale=ts[:, g * H + h, :],
                         start=(g == 0), stop=(g == GROUPS - 1),
                     )
-                copy_on(engines[i], out=o1_sb[h][:, c, e, m * DH : (m + 1) * DH], in_=acc[:])
-                if i == 1:
-                    flush()
-            view = out_1[h].rearrange("(c e q m) o -> c q e (m o)", c=2, e=E, m=W)[c]
-            if (h, c) == (1, 1):
-                nc.sync.dma_start(out=view[:, 0:2, :], in_=o1_sb[h][:, c, 0:2, :])
-                nc.scalar.dma_start(out=view[:, 2:4, :], in_=o1_sb[h][:, c, 2:4, :])
-            elif c == 0:
-                nc.sync.dma_start(out=view, in_=o1_sb[h][:, c, :, :])
-            else:
-                pending.append((view, o1_sb[h][:, c, :, :]))
+                copy_on(
+                    engines[e],
+                    out=o1[:, e, :].rearrange("p (w u e) -> p w u e", u=2, e=2),
+                    in_=acc[:].rearrange("p (u w e) -> p w u e", u=2, e=2),
+                )
+            nc.sync.dma_start(out=out_1[h].rearrange("(c e q) o -> c q e o", c=2, e=4)[c], in_=o1[:])
 
         with tc.manual_schedule():
+            load_w(0)
             open_group(0)
-            open_group(1)
             load_dz_rows(0, 0, 2)
             load_dz_rows(0, 2, 4)
-            load_w(0, 0)
-            load_w(0, 1)
+            load_w(1)
+            open_group(1)
             load_dz_rows(1, 0, 2)
-            load_w(1, 0)
-            load_w(1, 1)
             load_dz_rows(1, 2, 4)
             load_x(0)
             load_x(1)
-            make_dz(0, 0, 2)
-            turn_dz(0, 0, "ss")
-            make_dz(0, 2, 4)
-            turn_dz(0, 1, "ss")
-            lay_dz_tok(0, 0, "v")
-            quant_dz_feat(0, 0, 0)
-            quant_dz_feat(0, 0, 1)
-            lay_dz_tok(0, 1, "v")
+            turn_w(0)
+            make_dz(0, 0)
+            turn_dz(0, 0)
+            quant_w(0)
+            make_dz(0, 1)
+            quant_dz_feat(0, 0)
+            turn_dz(0, 1)
+            make_out0(0, 0, 0)
+            turn_w(1)
+            lay_dz_tok(0, 0)
+            quant_dz_feat(0, 1)
+            make_out0(0, 1, 0)
+            lay_dz_tok(0, 1)
+            make_dz(1, 0)
+            turn_dz(1, 0)
+            quant_w(1)
+            make_out0(0, 0, 1)
+            make_dz(1, 1)
             quant_dz_tok(0, 0)
-            quant_dz_feat(0, 1, 0)
-            quant_dz_feat(0, 1, 1)
-            turn_w(0, 0, "ss")
-            turn_w(0, 1, "ss")
-            quant_w(0, 0)
-            make_dz(1, 0, 2)
-            quant_w(0, 1)
+            turn_dz(1, 1)
+            make_out0(0, 1, 1)
             quant_dz_tok(0, 1)
-            turn_w(1, 0, "ss")
-            turn_w(1, 1, "ss")
-            quant_w(1, 0)
-            quant_w(1, 1)
-            turn_dz(1, 0, "ss")
-            make_dz(1, 2, 4)
-            make_out0(0, 0, "ssss")
-            make_out0(0, 1, "ssss")
-            turn_dz(1, 1, "ss")
-            lay_dz_tok(1, 0, "v")
-            quant_dz_feat(1, 0, 0)
-            quant_dz_feat(1, 0, 1)
-            make_out0(0, 2, "ssss")
-            lay_dz_tok(1, 1, "v")
+            lay_dz_tok(1, 0)
+            quant_dz_feat(1, 0)
+            make_out0(1, 0, 0)
+            lay_dz_tok(1, 1)
+            quant_dz_feat(1, 1)
+            make_out0(1, 0, 1)
+            make_out0(1, 1, 0)
+            make_out0(1, 1, 1)
             quant_dz_tok(1, 0)
-            quant_dz_feat(1, 1, 0)
-            quant_dz_feat(1, 1, 1)
-            make_out0(0, 3, "ssss")
-            lay_x(0, 0, "v")
+            lay_x(0, 0)
             quant_dz_tok(1, 1)
-            make_out0(1, 0, "ssss")
-            lay_x(0, 1, "v")
+            lay_x(1, 0)
             quant_x(0, 0)
-            make_out0(1, 1, "ssss")
-            lay_x(0, 2, "v")
-            quant_x(0, 1)
-            make_out0(1, 2, "ssss")
-            lay_x(0, 3, "v")
-            quant_x(0, 2)
-            make_out0(1, 3, "ssss")
-            lay_x(1, 0, "v")
-            quant_x(0, 3)
-            lay_x(1, 1, "v")
-            quant_x(1, 0)
-            make_out1(0, 0, "ssss")
-            lay_x(1, 2, "v")
-            quant_x(1, 1)
-            make_out1(0, 1, "ssss")
-            lay_x(1, 3, "v")
-            quant_x(1, 2)
-            make_out1(1, 0, "ssss")
+            for i in range(1, 4):
+                lay_x(0, i)
+                quant_x(1, i - 1)
+                make_out1(i - 1, "ssss")
+                lay_x(1, i)
+                quant_x(0, i)
             quant_x(1, 3)
-            make_out1(1, 1, "svsv")
+            make_out1(3, "svsv")

@@ -43,26 +43,31 @@ def tile_implicitrelationencoder_pb_v_kernel(
 
         ident = keep.tile([P, P], F32, name="ident")
         make_identity(nc, ident[:])
+        ident16 = keep.tile([P, P], BF16, name="ident16")
+        make_identity(nc, ident16[:])
 
         xq = keep.tile([P, GROUPS * H * 2, CHUNK], U32, name="xq", align_bytes=64)
         xs = keep.tile([P, GROUPS * H * 2, CHUNK], U8, name="xs", align_bytes=64)
         tq = keep.tile([P, GROUPS * H, CHUNK], U32, name="tq", align_bytes=64)
         ts = keep.tile([P, GROUPS * H, CHUNK], U8, name="ts", align_bytes=64)
-        fq = keep.tile([P, GROUPS * 2, CHUNK], U32, name="fq", align_bytes=64)
-        fs = keep.tile([P, GROUPS * 2, CHUNK], U8, name="fs", align_bytes=64)
+        fq = keep.tile([P, GROUPS * PACK, H * P], U32, name="fq", align_bytes=64)
+        fs = keep.tile([P, GROUPS * PACK, H * P], U8, name="fs", align_bytes=64)
         wq = keep.tile([P, H * 2, CHUNK], U32, name="wq", align_bytes=64)
         ws = keep.tile([P, H * 2, CHUNK], U8, name="ws", align_bytes=64)
 
-        z_sb, g_sb, w_sb, x_sb = {}, {}, {}, {}
+        z_sb, g_sb, w_sb, x_sb, dz_sb = {}, {}, {}, {}, {}
+        for g in range(GROUPS):
+            dz_sb[g] = keep.tile([P, PACK * H * DH], BF16, name="dz%d" % g, align_bytes=64)
 
-        def open_group(g):
-            z_sb[g] = work.tile([P, PACK, H * DH], F32, name="zt", tag="k16", bufs=6)
-            g_sb[g] = work.tile([P, PACK, H * DH], BF16, name="gt", tag="k8", bufs=4)
+        def load_z(g, lo, hi):
+            if lo == 0:
+                z_sb[g] = work.tile([P, PACK, H * DH], F32, name="zt", tag="k16", bufs=6)
+            nc.sync.dma_start(out=z_sb[g][:, lo:hi, :], in_=group_view(z_rows, g)[:, lo:hi, :])
 
-        def load_dz_rows(g, lo, hi):
-            js = slice(lo, hi)
-            nc.sync.dma_start(out=z_sb[g][:, js, :], in_=group_view(z_rows, g)[:, js, :])
-            nc.sync.dma_start(out=g_sb[g][:, js, :], in_=group_view(g_rows, g)[:, js, :])
+        def load_g(g, lo, hi):
+            if lo == 0:
+                g_sb[g] = work.tile([P, PACK, H * DH], BF16, name="gt", tag="k8", bufs=4)
+            nc.sync.dma_start(out=g_sb[g][:, lo:hi, :], in_=group_view(g_rows, g)[:, lo:hi, :])
 
         def load_w(h):
             w_sb[h] = work.tile([P, W_ROWS * DH], BF16, name="wt", tag="k8", bufs=4)
@@ -72,14 +77,14 @@ def tile_implicitrelationencoder_pb_v_kernel(
             x_sb[g] = work.tile([P, PACK, H * D], BF16, name="xt", tag="k16", bufs=6)
             nc.sync.dma_start(out=x_sb[g][:], in_=group_view(x_rows, g))
 
-        def make_dz(g, a):
-            js = slice(2 * a, 2 * a + 2)
+        def make_dz(g, lo, hi):
+            dst = dz_sb[g][:].rearrange("p (j h u w e) -> p u j h w e", j=PACK, h=H, u=2, e=2)
             for u in range(2):
                 nc.vector.scalar_tensor_tensor(
-                    out=dz_all[g][:, js, :].rearrange("p j (h u w e) -> p u j h w e", h=H, u=2, e=2)[:, u],
-                    in0=z_sb[g][:, js, :].rearrange("p j (h w u e) -> p u j h w e", h=H, u=2, e=2)[:, u],
+                    out=dst[:, u, lo:hi],
+                    in0=z_sb[g][:, lo:hi, :].rearrange("p j (h w u e) -> p u j h w e", h=H, u=2, e=2)[:, u],
                     scalar=0.0,
-                    in1=g_sb[g][:, js, :].rearrange("p j (h w u e) -> p u j h w e", h=H, u=2, e=2)[:, u],
+                    in1=g_sb[g][:, lo:hi, :].rearrange("p j (h w u e) -> p u j h w e", h=H, u=2, e=2)[:, u],
                     op0=GT, op1=MULT,
                 )
 
@@ -89,29 +94,30 @@ def tile_implicitrelationencoder_pb_v_kernel(
             else:
                 nc.scalar.copy(out=out, in_=in_)
 
-        dz_all = {}
-        for g in range(GROUPS):
-            dz_all[g] = keep.tile([P, PACK, H * DH], BF16, name="dz%d" % g, align_bytes=64)
-
         fgrp = {}
 
-        def turn_dz(g, a):
-            grp = work.tile([P, 2048], BF16, name="fgrp", tag="grp", bufs=3, align_bytes=64)
-            fgrp[g, a] = grp
-            words = dz_all[g][:].rearrange("p j w -> p (j w)").bitcast(F32)
-            for h in range(H):
-                tp = psum.tile([P, 4, P], F32, name="tp", tag="tp", bufs=3)
-                for jj in range(2):
-                    for u in range(2):
-                        off = (2 * a + jj) * 512 + h * 256 + u * P
-                        nc.tensor.transpose(tp[:, 2 * jj + u, :], words[:, off : off + P], ident[:])
-                nc.scalar.copy(
-                    out=grp[:].bitcast(F32)[:, h * 512 : (h + 1) * 512].rearrange("p (j r u) -> p j r u", j=2, u=2),
-                    in_=tp[:].rearrange("p (j u) r -> p j r u", u=2),
-                )
+        def turn_dz(g, j):
+            if j % 2 == 0:
+                fgrp[g, j // 2] = work.tile([P, 2048], BF16, name="fgrp", tag="grp", bufs=2, align_bytes=64)
+            words = dz_sb[g][:].bitcast(F32)
+            tp = psum.tile([P, 4, P], F32, name="tp", tag="tp", bufs=3)
+            for k in range(4):
+                off = (4 * j + k) * P
+                nc.tensor.transpose(tp[:, k, :], words[:, off : off + P], ident[:])
+            nc.scalar.copy(
+                out=fgrp[g, j // 2][:].bitcast(F32)[:, (j % 2) * 512 : (j % 2 + 1) * 512].rearrange(
+                    "p (h r u) -> p h r u", h=H, u=2
+                ),
+                in_=tp[:].rearrange("p (h u) r -> p h r u", u=2),
+            )
 
-        def quant_dz_feat(g, a):
-            nc.vector.quantize_mx(out=fq[:, 2 * g + a, :].bitcast(E5X4), scales=fs[:, 2 * g + a, :], in_=fgrp[g, a][:])
+        def quant_dz_feat(g, lo, hi):
+            rows = slice(PACK * g + lo, PACK * g + hi)
+            nc.vector.quantize_mx(
+                out=fq[:, rows, :].rearrange("p j n -> p (j n)").bitcast(E5X4),
+                scales=fs[:, rows, :].rearrange("p j n -> p (j n)"),
+                in_=fgrp[g, lo // 2][:, (lo % 2) * 1024 : (lo % 2 + hi - lo) * 1024],
+            )
 
         wgrp = {}
 
@@ -135,52 +141,70 @@ def tile_implicitrelationencoder_pb_v_kernel(
                 in_=wgrp[h][:],
             )
 
+        def interleave(src, how):
+            grp = work.tile([P, 2048], BF16, name="grp", tag="il", bufs=4, align_bytes=64)
+            if how == "v":
+                nc.vector.tensor_copy(
+                    out=grp[:].rearrange("p (c i j) -> p c j i", i=4, j=PACK),
+                    in_=src.rearrange("p j (c i) -> p c j i", i=4),
+                )
+                return grp
+            for half in range(2):
+                tp = psum.tile([P, 2, CHUNK], BF16, name="tp", tag="tp", bufs=3)
+                for k in range(2):
+                    lo = (2 * half + k) * P
+                    nc.tensor.matmul(
+                        out=tp[:, k, :], lhsT=ident16[:],
+                        rhs=src[:, :, lo : lo + P].rearrange("p j c -> p c j"), start=True, stop=True,
+                    )
+                copy_on(
+                    how[half],
+                    out=grp[:, half * 1024 : (half + 1) * 1024].bitcast(F32),
+                    in_=tp[:].rearrange("p k n -> p (k n)").bitcast(F32),
+                )
+            return grp
+
         tgrp = {}
 
-        def lay_dz_tok(g, h):
-            grp = work.tile([P, 2048], BF16, name="tgrp", tag="il", bufs=3, align_bytes=64)
-            tgrp[g, h] = grp
-            nc.vector.tensor_copy(
-                out=grp[:].rearrange("p (c i j) -> p c j i", i=4, j=PACK),
-                in_=dz_all[g][:, :, h * DH : (h + 1) * DH].rearrange("p j (c i) -> p c j i", i=4),
-            )
+        def lay_dz_tok(g, h, how):
+            tgrp[g, h] = interleave(dz_sb[g][:].rearrange("p (j n) -> p j n", j=PACK)[:, :, h * DH : (h + 1) * DH], how)
 
         def quant_dz_tok(g, h):
             nc.vector.quantize_mx(out=tq[:, g * H + h, :].bitcast(E5X4), scales=ts[:, g * H + h, :], in_=tgrp[g, h][:])
 
         xgrp = {}
 
-        def lay_x(g, i):
-            grp = work.tile([P, 2048], BF16, name="xgrp", tag="il", bufs=3, align_bytes=64)
-            xgrp[g, i] = grp
-            nc.vector.tensor_copy(
-                out=grp[:].rearrange("p (c i j) -> p c j i", i=4, j=PACK),
-                in_=x_sb[g][:, :, i * CHUNK : (i + 1) * CHUNK].rearrange("p j (c i) -> p c j i", i=4),
-            )
+        def lay_x(g, i, how):
+            xgrp[g, i] = interleave(x_sb[g][:, :, i * CHUNK : (i + 1) * CHUNK], how)
 
         def quant_x(g, i):
             nc.vector.quantize_mx(out=xq[:, g * 4 + i, :].bitcast(E4X4), scales=xs[:, g * 4 + i, :], in_=xgrp[g, i][:])
 
         o0_sb = {}
 
-        def make_out0(g, a, h):
-            if h == 0:
-                o0_sb[g, a] = work.tile([P, 2, H * D], F32, name="o0", tag="k16", bufs=6)
-            for jj in range(2):
-                rows = slice(h * 256 + jj * P, h * 256 + (jj + 1) * P)
-                for c in range(2):
-                    acc = psum.tile([P, CHUNK], F32, name="acc", tag="acc", bufs=5)
-                    nc.tensor.matmul_mx(
-                        out=acc[:],
-                        lhsT=fq[:, 2 * g + a, rows].bitcast(E5X4), lhsT_scale=fs[:, 2 * g + a, rows],
-                        rhs=wq[:, 2 * h + c, :].bitcast(E4X4), rhs_scale=ws[:, 2 * h + c, :],
-                        start=True, stop=True,
-                    )
-                    nc.scalar.copy(out=o0_sb[g, a][:, jj, (2 * h + c) * CHUNK : (2 * h + c + 1) * CHUNK], in_=acc[:])
-            if h == H - 1:
-                nc.sync.dma_start(out=group_view(o0_rows, g)[:, 2 * a : 2 * a + 2, :], in_=o0_sb[g, a][:])
+        def make_out0(g, j, h, engines="ss"):
+            if (g, j // 2) not in o0_sb:
+                o0_sb[g, j // 2] = work.tile([P, 2, H * D], F32, name="o0", tag="k16", bufs=6)
+            rows = slice(h * P, (h + 1) * P)
+            for c in range(2):
+                acc = psum.tile([P, CHUNK], F32, name="acc", tag="acc", bufs=5)
+                nc.tensor.matmul_mx(
+                    out=acc[:],
+                    lhsT=fq[:, PACK * g + j, rows].bitcast(E5X4), lhsT_scale=fs[:, PACK * g + j, rows],
+                    rhs=wq[:, 2 * h + c, :].bitcast(E4X4), rhs_scale=ws[:, 2 * h + c, :],
+                    start=True, stop=True,
+                )
+                copy_on(
+                    engines[c],
+                    out=o0_sb[g, j // 2][:, j % 2, (2 * h + c) * CHUNK : (2 * h + c + 1) * CHUNK], in_=acc[:],
+                )
 
-        def make_out1(i, engines):
+        def store_out0(g, lo, hi):
+            nc.sync.dma_start(
+                out=group_view(o0_rows, g)[:, lo:hi, :], in_=o0_sb[g, lo // 2][:, lo % 2 : lo % 2 + hi - lo, :]
+            )
+
+        def make_out1(i, engines, pieces=1):
             h, c = divmod(i, 2)
             o1 = work.tile([P, 4, DH], F32, name="o1", tag="k8", bufs=4)
             for e in range(4):
@@ -198,59 +222,83 @@ def tile_implicitrelationencoder_pb_v_kernel(
                     out=o1[:, e, :].rearrange("p (w u e) -> p w u e", u=2, e=2),
                     in_=acc[:].rearrange("p (u w e) -> p w u e", u=2, e=2),
                 )
-            nc.sync.dma_start(out=out_1[h].rearrange("(c e q) o -> c q e o", c=2, e=4)[c], in_=o1[:])
+                if (e + 1) % (4 // pieces) == 0:
+                    es = slice(e + 1 - 4 // pieces, e + 1)
+                    nc.sync.dma_start(
+                        out=out_1[h].rearrange("(c e q) o -> c q e o", c=2, e=4)[c][:, es, :], in_=o1[:, es, :]
+                    )
 
         with tc.manual_schedule():
             load_w(0)
-            open_group(0)
-            load_dz_rows(0, 0, 2)
-            load_dz_rows(0, 2, 4)
+            load_z(0, 0, 1)
+            load_g(0, 0, 2)
+            load_z(0, 1, 2)
+            load_z(0, 2, 4)
+            load_g(0, 2, 4)
             load_w(1)
-            open_group(1)
-            load_dz_rows(1, 0, 2)
-            load_dz_rows(1, 2, 4)
+            load_z(1, 0, 2)
+            load_g(1, 0, 4)
+            load_z(1, 2, 4)
             load_x(0)
             load_x(1)
             turn_w(0)
-            make_dz(0, 0)
+            make_dz(0, 0, 1)
             turn_dz(0, 0)
-            quant_w(0)
-            make_dz(0, 1)
-            quant_dz_feat(0, 0)
+            make_dz(0, 1, 2)
             turn_dz(0, 1)
+            quant_w(0)
+            quant_dz_feat(0, 0, 2)
             make_out0(0, 0, 0)
-            turn_w(1)
-            lay_dz_tok(0, 0)
-            quant_dz_feat(0, 1)
             make_out0(0, 1, 0)
-            lay_dz_tok(0, 1)
-            make_dz(1, 0)
-            turn_dz(1, 0)
-            quant_w(1)
-            make_out0(0, 0, 1)
-            make_dz(1, 1)
+            make_dz(0, 2, 4)
+            turn_dz(0, 2)
+            turn_dz(0, 3)
+            turn_w(1)
+            lay_dz_tok(0, 0, "v")
+            quant_dz_feat(0, 2, 4)
+            make_out0(0, 2, 0)
+            make_out0(0, 3, 0)
+            lay_dz_tok(0, 1, "v")
             quant_dz_tok(0, 0)
-            turn_dz(1, 1)
+            quant_w(1)
+            make_dz(1, 0, 2)
+            make_out0(0, 0, 1)
             make_out0(0, 1, 1)
+            store_out0(0, 0, 2)
+            turn_dz(1, 0)
+            turn_dz(1, 1)
+            make_dz(1, 2, 4)
+            make_out0(0, 2, 1)
+            make_out0(0, 3, 1)
+            store_out0(0, 2, 4)
+            turn_dz(1, 2)
+            turn_dz(1, 3)
+            quant_dz_feat(1, 0, 2)
             quant_dz_tok(0, 1)
-            lay_dz_tok(1, 0)
-            quant_dz_feat(1, 0)
-            make_out0(1, 0, 0)
-            lay_dz_tok(1, 1)
-            quant_dz_feat(1, 1)
-            make_out0(1, 0, 1)
-            make_out0(1, 1, 0)
-            make_out0(1, 1, 1)
+            for j in range(2):
+                for h in range(H):
+                    make_out0(1, j, h)
+            store_out0(1, 0, 2)
+            lay_dz_tok(1, 0, "v")
+            quant_dz_feat(1, 2, 4)
+            lay_dz_tok(1, 1, "v")
             quant_dz_tok(1, 0)
-            lay_x(0, 0)
+            lay_x(0, 0, "v")
             quant_dz_tok(1, 1)
-            lay_x(1, 0)
+            for h in range(H):
+                make_out0(1, 2, h)
+            lay_x(1, 0, "ss")
+            for h in range(H):
+                make_out0(1, 3, h)
+            store_out0(1, 2, 4)
+            lay_x(0, 1, "v")
             quant_x(0, 0)
+            quant_x(1, 0)
             for i in range(1, 4):
-                lay_x(0, i)
-                quant_x(1, i - 1)
-                make_out1(i - 1, "ssss")
-                lay_x(1, i)
+                lay_x(1, i, "ss")
+                if i < 3:
+                    lay_x(0, i + 1, "v")
                 quant_x(0, i)
-            quant_x(1, 3)
-            make_out1(3, "svsv")
+                quant_x(1, i)
+                make_out1(i - 1, "vsss" if i < 3 else "vsvs")
+            make_out1(3, "vsvs", 2)

@@ -43,8 +43,6 @@ def tile_implicitrelationencoder_pb_v_kernel(
 
         ident = keep.tile([P, P], F32, name="ident")
         make_identity(nc, ident[:])
-        ident16 = keep.tile([P, P], BF16, name="ident16")
-        make_identity(nc, ident16[:])
 
         xq = keep.tile([P, GROUPS * H * 2, CHUNK], U32, name="xq", align_bytes=64)
         xs = keep.tile([P, GROUPS * H * 2, CHUNK], U8, name="xs", align_bytes=64)
@@ -100,7 +98,7 @@ def tile_implicitrelationencoder_pb_v_kernel(
             if j % 2 == 0:
                 fgrp[g, j // 2] = work.tile([P, 2048], BF16, name="fgrp", tag="grp", bufs=2, align_bytes=64)
             words = dz_sb[g][:].bitcast(F32)
-            tp = psum.tile([P, 4, P], F32, name="tp", tag="tp", bufs=3)
+            tp = psum.tile([P, 4, P], F32, name="tp", tag="bank", bufs=8)
             for k in range(4):
                 off = (4 * j + k) * P
                 nc.tensor.transpose(tp[:, k, :], words[:, off : off + P], ident[:])
@@ -127,7 +125,7 @@ def tile_implicitrelationencoder_pb_v_kernel(
             words = w_sb[h][:].bitcast(F32)
             dst = grp[:].bitcast(F32).rearrange("p (q k) -> p q k", k=2 * W_ROWS)
             for mm in range(W_ROWS // 2):
-                tp = psum.tile([P, 4, P], F32, name="tp", tag="tp", bufs=3)
+                tp = psum.tile([P, 4, P], F32, name="tp", tag="bank", bufs=8)
                 for i in range(2):
                     for u in range(2):
                         off = (2 * mm + i) * 256
@@ -141,27 +139,13 @@ def tile_implicitrelationencoder_pb_v_kernel(
                 in_=wgrp[h][:],
             )
 
-        def interleave(src, how):
-            grp = work.tile([P, 2048], BF16, name="grp", tag="il", bufs=4, align_bytes=64)
-            if how == "v":
-                nc.vector.tensor_copy(
-                    out=grp[:].rearrange("p (c i j) -> p c j i", i=4, j=PACK),
-                    in_=src.rearrange("p j (c i) -> p c j i", i=4),
-                )
-                return grp
-            for half in range(2):
-                tp = psum.tile([P, 2, CHUNK], BF16, name="tp", tag="tp", bufs=3)
-                for k in range(2):
-                    lo = (2 * half + k) * P
-                    nc.tensor.matmul(
-                        out=tp[:, k, :], lhsT=ident16[:],
-                        rhs=src[:, :, lo : lo + P].rearrange("p j c -> p c j"), start=True, stop=True,
-                    )
-                copy_on(
-                    how[half],
-                    out=grp[:, half * 1024 : (half + 1) * 1024].bitcast(F32),
-                    in_=tp[:].rearrange("p k n -> p (k n)").bitcast(F32),
-                )
+        def interleave(src, engine):
+            grp = work.tile([P, 2048], BF16, name="grp", tag="il_" + engine, bufs=3 if engine == "v" else 1, align_bytes=64)
+            copy_on(
+                engine,
+                out=grp[:].rearrange("p (c i j) -> p c j i", i=4, j=PACK),
+                in_=src.rearrange("p j (c i) -> p c j i", i=4),
+            )
             return grp
 
         tgrp = {}
@@ -187,7 +171,7 @@ def tile_implicitrelationencoder_pb_v_kernel(
                 o0_sb[g, j // 2] = work.tile([P, 2, H * D], F32, name="o0", tag="k16", bufs=6)
             rows = slice(h * P, (h + 1) * P)
             for c in range(2):
-                acc = psum.tile([P, CHUNK], F32, name="acc", tag="acc", bufs=5)
+                acc = psum.tile([P, CHUNK], F32, name="acc", tag="bank", bufs=8)
                 nc.tensor.matmul_mx(
                     out=acc[:],
                     lhsT=fq[:, PACK * g + j, rows].bitcast(E5X4), lhsT_scale=fs[:, PACK * g + j, rows],
@@ -204,23 +188,32 @@ def tile_implicitrelationencoder_pb_v_kernel(
                 out=group_view(o0_rows, g)[:, lo:hi, :], in_=o0_sb[g, lo // 2][:, lo % 2 : lo % 2 + hi - lo, :]
             )
 
-        def make_out1(i, engines, pieces=1):
+        o1_acc = {}
+
+        def pass_out1(i, g, e):
+            cols = slice(e * P, (e + 1) * P)
+            if g == 0:
+                o1_acc[i, e] = psum.tile([P, CHUNK], F32, name="acc", tag="bank", bufs=8)
+            nc.tensor.matmul_mx(
+                out=o1_acc[i, e][:],
+                lhsT=xq[:, g * 4 + i, cols].bitcast(E4X4), lhsT_scale=xs[:, g * 4 + i, cols],
+                rhs=tq[:, g * H + i // 2, :].bitcast(E5X4), rhs_scale=ts[:, g * H + i // 2, :],
+                start=(g == 0), stop=(g == GROUPS - 1),
+            )
+
+        def open_out1(i):
+            for e in range(4):
+                pass_out1(i, 0, e)
+
+        def close_out1(i, engines, pieces=1):
             h, c = divmod(i, 2)
             o1 = work.tile([P, 4, DH], F32, name="o1", tag="k8", bufs=4)
             for e in range(4):
-                cols = slice(e * P, (e + 1) * P)
-                acc = psum.tile([P, CHUNK], F32, name="acc", tag="acc", bufs=5)
-                for g in range(GROUPS):
-                    nc.tensor.matmul_mx(
-                        out=acc[:],
-                        lhsT=xq[:, g * 4 + i, cols].bitcast(E4X4), lhsT_scale=xs[:, g * 4 + i, cols],
-                        rhs=tq[:, g * H + h, :].bitcast(E5X4), rhs_scale=ts[:, g * H + h, :],
-                        start=(g == 0), stop=(g == GROUPS - 1),
-                    )
+                pass_out1(i, 1, e)
                 copy_on(
                     engines[e],
                     out=o1[:, e, :].rearrange("p (w u e) -> p w u e", u=2, e=2),
-                    in_=acc[:].rearrange("p (u w e) -> p w u e", u=2, e=2),
+                    in_=o1_acc[i, e][:].rearrange("p (u w e) -> p w u e", u=2, e=2),
                 )
                 if (e + 1) % (4 // pieces) == 0:
                     es = slice(e + 1 - 4 // pieces, e + 1)
@@ -236,9 +229,8 @@ def tile_implicitrelationencoder_pb_v_kernel(
             load_z(0, 2, 4)
             load_g(0, 2, 4)
             load_w(1)
-            load_z(1, 0, 2)
             load_g(1, 0, 4)
-            load_z(1, 2, 4)
+            load_z(1, 0, 4)
             load_x(0)
             load_x(1)
             turn_w(0)
@@ -255,11 +247,12 @@ def tile_implicitrelationencoder_pb_v_kernel(
             turn_dz(0, 3)
             turn_w(1)
             lay_dz_tok(0, 0, "v")
+            lay_dz_tok(0, 1, "v")
             quant_dz_feat(0, 2, 4)
             make_out0(0, 2, 0)
             make_out0(0, 3, 0)
-            lay_dz_tok(0, 1, "v")
             quant_dz_tok(0, 0)
+            quant_dz_tok(0, 1)
             quant_w(1)
             make_dz(1, 0, 2)
             make_out0(0, 0, 1)
@@ -274,31 +267,28 @@ def tile_implicitrelationencoder_pb_v_kernel(
             turn_dz(1, 2)
             turn_dz(1, 3)
             quant_dz_feat(1, 0, 2)
-            quant_dz_tok(0, 1)
             for j in range(2):
                 for h in range(H):
                     make_out0(1, j, h)
             store_out0(1, 0, 2)
             lay_dz_tok(1, 0, "v")
-            quant_dz_feat(1, 2, 4)
             lay_dz_tok(1, 1, "v")
+            quant_dz_feat(1, 2, 4)
+            for j in range(2, 4):
+                for h in range(H):
+                    make_out0(1, j, h)
+            store_out0(1, 2, 4)
             quant_dz_tok(1, 0)
             lay_x(0, 0, "v")
             quant_dz_tok(1, 1)
-            for h in range(H):
-                make_out0(1, 2, h)
-            lay_x(1, 0, "ss")
-            for h in range(H):
-                make_out0(1, 3, h)
-            store_out0(1, 2, 4)
-            lay_x(0, 1, "v")
-            quant_x(0, 0)
-            quant_x(1, 0)
-            for i in range(1, 4):
-                lay_x(1, i, "ss")
+            for i in range(4):
+                if i != 2:
+                    lay_x(1, i, "v")
+                quant_x(0, i)
+                if i == 0:
+                    lay_x(1, 2, "s")
+                open_out1(i)
                 if i < 3:
                     lay_x(0, i + 1, "v")
-                quant_x(0, i)
                 quant_x(1, i)
-                make_out1(i - 1, "vsss" if i < 3 else "vsvs")
-            make_out1(3, "vsvs", 2)
+                close_out1(i, "ssss" if i < 3 else "vsvs", 1 if i < 3 else 2)

@@ -139,19 +139,21 @@ def tile_implicitrelationencoder_pb_v_kernel(
                 in_=wgrp[h][:],
             )
 
-        def interleave(src, engine):
+        def interleave(src, engine, rows):
             grp = work.tile([P, 2048], BF16, name="grp", tag="il_" + engine, bufs=3 if engine == "v" else 1, align_bytes=64)
-            copy_on(
-                engine,
-                out=grp[:].rearrange("p (c i j) -> p c j i", i=4, j=PACK),
-                in_=src.rearrange("p j (c i) -> p c j i", i=4),
-            )
+            if rows == 1:
+                dst = grp[:].rearrange("p (c i j) -> p c j i", i=4, j=PACK)
+                src = src.rearrange("p j (c i) -> p c j i", i=4)
+            else:
+                dst = grp[:].rearrange("p (m c s j) -> p c j s m", m=2, s=2, j=PACK)
+                src = src.rearrange("p j (c s m) -> p c j s m", s=2, m=2)
+            copy_on(engine, out=dst, in_=src)
             return grp
 
         tgrp = {}
 
         def lay_dz_tok(g, h, how):
-            tgrp[g, h] = interleave(dz_sb[g][:].rearrange("p (j n) -> p j n", j=PACK)[:, :, h * DH : (h + 1) * DH], how)
+            tgrp[g, h] = interleave(dz_sb[g][:].rearrange("p (j n) -> p j n", j=PACK)[:, :, h * DH : (h + 1) * DH], how, 1)
 
         def quant_dz_tok(g, h):
             nc.vector.quantize_mx(out=tq[:, g * H + h, :].bitcast(E5X4), scales=ts[:, g * H + h, :], in_=tgrp[g, h][:])
@@ -159,7 +161,7 @@ def tile_implicitrelationencoder_pb_v_kernel(
         xgrp = {}
 
         def lay_x(g, i, how):
-            xgrp[g, i] = interleave(x_sb[g][:, :, i * CHUNK : (i + 1) * CHUNK], how)
+            xgrp[g, i] = interleave(x_sb[g][:, :, i * CHUNK : (i + 1) * CHUNK], how, 2)
 
         def quant_x(g, i):
             nc.vector.quantize_mx(out=xq[:, g * 4 + i, :].bitcast(E4X4), scales=xs[:, g * 4 + i, :], in_=xgrp[g, i][:])
@@ -191,7 +193,8 @@ def tile_implicitrelationencoder_pb_v_kernel(
         o1_acc = {}
 
         def pass_out1(i, g, e):
-            cols = slice(e * P, (e + 1) * P)
+            a, m = divmod(e, 2)
+            cols = slice((2 * m + a) * P, (2 * m + a + 1) * P)
             if g == 0:
                 o1_acc[i, e] = psum.tile([P, CHUNK], F32, name="acc", tag="bank", bufs=8)
             nc.tensor.matmul_mx(
@@ -216,9 +219,10 @@ def tile_implicitrelationencoder_pb_v_kernel(
                     in_=o1_acc[i, e][:].rearrange("p (u w e) -> p w u e", u=2, e=2),
                 )
                 if (e + 1) % (4 // pieces) == 0:
-                    es = slice(e + 1 - 4 // pieces, e + 1)
+                    es = slice((e + 1 - 4 // pieces) // 2, (e + 1) // 2)
                     nc.sync.dma_start(
-                        out=out_1[h].rearrange("(c e q) o -> c q e o", c=2, e=4)[c][:, es, :], in_=o1[:, es, :]
+                        out=out_1[h].rearrange("(c a q m) o -> c q a (m o)", c=2, a=2, m=2)[c][:, es, :],
+                        in_=o1[:].rearrange("p (a m) o -> p a (m o)", m=2)[:, es, :],
                     )
 
         with tc.manual_schedule():

@@ -59,20 +59,20 @@ def tile_implicitrelationencoder_pb_v_kernel(
 
         def load_z(g, lo, hi):
             if lo == 0:
-                z_sb[g] = work.tile([P, PACK, H * DH], F32, name="zt", tag="k16", bufs=6)
+                z_sb[g] = work.tile([P, PACK, H * DH], F32, name="zt", tag="k16", bufs=6, align_bytes=256)
             nc.sync.dma_start(out=z_sb[g][:, lo:hi, :], in_=group_view(z_rows, g)[:, lo:hi, :])
 
         def load_g(g, lo, hi):
             if lo == 0:
-                g_sb[g] = work.tile([P, PACK, H * DH], BF16, name="gt", tag="k8", bufs=4)
+                g_sb[g] = work.tile([P, PACK, H * DH], BF16, name="gt", tag="k8", bufs=4, align_bytes=256)
             nc.sync.dma_start(out=g_sb[g][:, lo:hi, :], in_=group_view(g_rows, g)[:, lo:hi, :])
 
         def load_w(h):
-            w_sb[h] = work.tile([P, W_ROWS * DH], BF16, name="wt", tag="k8", bufs=4)
+            w_sb[h] = work.tile([P, W_ROWS * DH], BF16, name="wt", tag="k8", bufs=4, align_bytes=256)
             nc.sync.dma_start(out=w_sb[h][:], in_=out_w[h].rearrange("(q m) o -> q (m o)", m=W_ROWS))
 
         def load_x(g):
-            x_sb[g] = work.tile([P, PACK, H * D], BF16, name="xt", tag="k16", bufs=6)
+            x_sb[g] = work.tile([P, PACK, H * D], BF16, name="xt", tag="k16", bufs=6, align_bytes=256)
             nc.sync.dma_start(out=x_sb[g][:], in_=group_view(x_rows, g))
 
         def make_dz(g, lo, hi):
@@ -170,7 +170,7 @@ def tile_implicitrelationencoder_pb_v_kernel(
 
         def make_out0(g, j, h, engines="ss"):
             if (g, j // 2) not in o0_sb:
-                o0_sb[g, j // 2] = work.tile([P, 2, H * D], F32, name="o0", tag="k16", bufs=6)
+                o0_sb[g, j // 2] = work.tile([P, 2, H * D], F32, name="o0", tag="k16", bufs=6, align_bytes=256)
             rows = slice(h * P, (h + 1) * P)
             for c in range(2):
                 acc = psum.tile([P, CHUNK], F32, name="acc", tag="bank", bufs=8)
@@ -210,7 +210,7 @@ def tile_implicitrelationencoder_pb_v_kernel(
 
         def close_out1(i, engines, pieces=1):
             h, c = divmod(i, 2)
-            o1 = work.tile([P, 4, DH], F32, name="o1", tag="k8", bufs=4)
+            o1 = work.tile([P, 4, DH], F32, name="o1", tag="k8", bufs=4, align_bytes=256)
             for e in range(4):
                 pass_out1(i, 1, e)
                 copy_on(

@@ -67,9 +67,13 @@ def tile_implicitrelationencoder_pb_v_kernel(
                 g_sb[g] = work.tile([P, PACK, H * DH], BF16, name="gt", tag="k8", bufs=4, align_bytes=256)
             nc.sync.dma_start(out=g_sb[g][:, lo:hi, :], in_=group_view(g_rows, g)[:, lo:hi, :])
 
-        def load_w(h):
-            w_sb[h] = work.tile([P, W_ROWS * DH], BF16, name="wt", tag="k8", bufs=4, align_bytes=256)
-            nc.sync.dma_start(out=w_sb[h][:], in_=out_w[h].rearrange("(q m) o -> q (m o)", m=W_ROWS))
+        def load_w(h, lo, hi):
+            if lo == 0:
+                w_sb[h] = work.tile([P, 2, PACK * DH], BF16, name="wt", tag="k8", bufs=4, align_bytes=256)
+            nc.sync.dma_start(
+                out=w_sb[h][:, lo:hi, :],
+                in_=out_w[h].rearrange("(c q m) o -> q c (m o)", c=2, m=PACK)[:, lo:hi, :],
+            )
 
         def load_x(g):
             x_sb[g] = work.tile([P, PACK, H * D], BF16, name="xt", tag="k16", bufs=6, align_bytes=256)
@@ -96,7 +100,7 @@ def tile_implicitrelationencoder_pb_v_kernel(
 
         def turn_dz(g, j):
             if j % 2 == 0:
-                fgrp[g, j // 2] = work.tile([P, 2048], BF16, name="fgrp", tag="grp", bufs=2, align_bytes=64)
+                fgrp[g, j // 2] = work.tile([P, 2048], BF16, name="fgrp", tag="grp", bufs=3, align_bytes=64)
             words = dz_sb[g][:].bitcast(F32)
             tp = psum.tile([P, 4, P], F32, name="tp", tag="bank", bufs=8)
             for k in range(4):
@@ -119,25 +123,20 @@ def tile_implicitrelationencoder_pb_v_kernel(
 
         wgrp = {}
 
-        def turn_w(h):
-            grp = work.tile([P, 4096], BF16, name="wgrp", tag="wgrp", bufs=2, align_bytes=64)
-            wgrp[h] = grp
-            words = w_sb[h][:].bitcast(F32)
-            dst = grp[:].bitcast(F32).rearrange("p (q k) -> p q k", k=2 * W_ROWS)
-            for mm in range(W_ROWS // 2):
-                tp = psum.tile([P, 4, P], F32, name="tp", tag="bank", bufs=8)
-                for i in range(2):
-                    for u in range(2):
-                        off = (2 * mm + i) * 256
-                        nc.tensor.transpose(tp[:, 2 * i + u, :], words[:, off + u : off + 256 : 2], ident[:])
-                nc.scalar.copy(out=dst[:, :, 4 * mm : 4 * mm + 4], in_=tp[:].rearrange("p k q -> p q k"))
+        def turn_w(h, c, mm):
+            if mm == 0:
+                wgrp[h, c] = work.tile([P, 2048], BF16, name="wgrp", tag="wgrp", bufs=3, align_bytes=64)
+            words = w_sb[h][:, c, :].bitcast(F32)
+            dst = wgrp[h, c][:].bitcast(F32).rearrange("p (q k) -> p q k", k=2 * PACK)
+            tp = psum.tile([P, 4, P], F32, name="tp", tag="bank", bufs=8)
+            for i in range(2):
+                for u in range(2):
+                    off = (2 * mm + i) * 256
+                    nc.tensor.transpose(tp[:, 2 * i + u, :], words[:, off + u : off + 256 : 2], ident[:])
+            nc.scalar.copy(out=dst[:, :, 4 * mm : 4 * mm + 4], in_=tp[:].rearrange("p k q -> p q k"))
 
-        def quant_w(h):
-            nc.vector.quantize_mx(
-                out=wq[:, 2 * h : 2 * h + 2, :].rearrange("p c n -> p (c n)").bitcast(E4X4),
-                scales=ws[:, 2 * h : 2 * h + 2, :].rearrange("p c n -> p (c n)"),
-                in_=wgrp[h][:],
-            )
+        def quant_w(h, c):
+            nc.vector.quantize_mx(out=wq[:, 2 * h + c, :].bitcast(E4X4), scales=ws[:, 2 * h + c, :], in_=wgrp[h, c][:])
 
         def interleave(src, engine, rows):
             grp = work.tile([P, 2048], BF16, name="grp", tag="il_" + engine, bufs=3 if engine == "v" else 1, align_bytes=64)
@@ -168,11 +167,11 @@ def tile_implicitrelationencoder_pb_v_kernel(
 
         o0_sb = {}
 
-        def make_out0(g, j, h, engines="ss"):
+        def make_out0(g, j, h, cs=(0, 1), engines="ss"):
             if (g, j // 2) not in o0_sb:
                 o0_sb[g, j // 2] = work.tile([P, 2, H * D], F32, name="o0", tag="k16", bufs=6, align_bytes=256)
             rows = slice(h * P, (h + 1) * P)
-            for c in range(2):
+            for c in cs:
                 acc = psum.tile([P, CHUNK], F32, name="acc", tag="bank", bufs=8)
                 nc.tensor.matmul_mx(
                     out=acc[:],
@@ -208,10 +207,12 @@ def tile_implicitrelationencoder_pb_v_kernel(
             for e in range(4):
                 pass_out1(i, 0, e)
 
-        def close_out1(i, engines, pieces=1):
+        def close_out1(i, engines, pieces=1, both=False):
             h, c = divmod(i, 2)
             o1 = work.tile([P, 4, DH], F32, name="o1", tag="k8", bufs=4, align_bytes=256)
             for e in range(4):
+                if both:
+                    pass_out1(i, 0, e)
                 pass_out1(i, 1, e)
                 copy_on(
                     engines[e],
@@ -226,73 +227,99 @@ def tile_implicitrelationencoder_pb_v_kernel(
                     )
 
         with tc.manual_schedule():
-            load_w(0)
+            load_w(0, 0, 2)
             load_z(0, 0, 1)
             load_g(0, 0, 2)
             load_z(0, 1, 2)
             load_z(0, 2, 4)
             load_g(0, 2, 4)
-            load_w(1)
+            load_w(1, 0, 2)
             load_g(1, 0, 4)
             load_z(1, 0, 4)
             load_x(0)
             load_x(1)
-            turn_w(0)
+            turn_w(0, 0, 0)
+            turn_w(0, 0, 1)
+            turn_w(0, 1, 0)
+            turn_w(0, 1, 1)
             make_dz(0, 0, 1)
+            quant_w(0, 0)
             turn_dz(0, 0)
             make_dz(0, 1, 2)
             turn_dz(0, 1)
-            quant_w(0)
-            quant_dz_feat(0, 0, 2)
+            quant_w(0, 1)
+            quant_dz_feat(0, 0, 1)
+            make_dz(0, 2, 3)
             make_out0(0, 0, 0)
-            make_out0(0, 1, 0)
-            make_dz(0, 2, 4)
             turn_dz(0, 2)
+            quant_dz_feat(0, 1, 2)
+            make_dz(0, 3, 4)
+            make_out0(0, 1, 0)
             turn_dz(0, 3)
-            turn_w(1)
-            lay_dz_tok(0, 0, "v")
-            lay_dz_tok(0, 1, "v")
-            quant_dz_feat(0, 2, 4)
+            quant_dz_feat(0, 2, 3)
+            turn_w(1, 0, 0)
             make_out0(0, 2, 0)
+            lay_dz_tok(0, 0, "v")
+            quant_dz_feat(0, 3, 4)
+            turn_w(1, 0, 1)
+            turn_w(1, 1, 0)
             make_out0(0, 3, 0)
+            turn_w(1, 1, 1)
+            lay_dz_tok(0, 1, "v")
             quant_dz_tok(0, 0)
+            quant_w(1, 0)
             quant_dz_tok(0, 1)
-            quant_w(1)
-            make_dz(1, 0, 2)
-            make_out0(0, 0, 1)
-            make_out0(0, 1, 1)
-            store_out0(0, 0, 2)
+            make_dz(1, 0, 1)
+            quant_w(1, 1)
+            make_dz(1, 1, 2)
+            make_out0(0, 0, 1, (0,))
+            make_out0(0, 1, 1, (0,))
+            make_out0(0, 2, 1, (0,))
             turn_dz(1, 0)
+            make_out0(0, 0, 1, (1,))
+            make_out0(0, 1, 1, (1,))
+            store_out0(0, 0, 2)
             turn_dz(1, 1)
             make_dz(1, 2, 4)
-            make_out0(0, 2, 1)
-            make_out0(0, 3, 1)
-            store_out0(0, 2, 4)
+            make_out0(0, 2, 1, (1,))
+            make_out0(0, 3, 1, (0,))
+            lay_dz_tok(1, 0, "v")
+            quant_dz_feat(1, 0, 2)
             turn_dz(1, 2)
             turn_dz(1, 3)
-            quant_dz_feat(1, 0, 2)
-            for j in range(2):
-                for h in range(H):
-                    make_out0(1, j, h)
-            store_out0(1, 0, 2)
-            lay_dz_tok(1, 0, "v")
-            lay_dz_tok(1, 1, "v")
-            quant_dz_feat(1, 2, 4)
-            for j in range(2, 4):
-                for h in range(H):
-                    make_out0(1, j, h)
-            store_out0(1, 2, 4)
+            make_out0(0, 3, 1, (1,))
+            store_out0(0, 2, 4)
             quant_dz_tok(1, 0)
             lay_x(0, 0, "v")
+            quant_dz_feat(1, 2, 4)
+            make_out0(1, 0, 0)
+            make_out0(1, 0, 1)
+            make_out0(1, 1, 0)
+            make_out0(1, 1, 1)
+            store_out0(1, 0, 2)
+            lay_x(1, 0, "v")
+            quant_x(0, 0)
+            quant_x(1, 0)
+            make_out0(1, 2, 0, engines="vs")
+            make_out0(1, 2, 1)
+            make_out0(1, 3, 0)
+            make_out0(1, 3, 1)
+            store_out0(1, 2, 4)
+            close_out1(0, "ssss", 1, True)
+            lay_x(0, 1, "v")
+            lay_x(1, 1, "v")
+            quant_x(0, 1)
+            quant_x(1, 1)
+            close_out1(1, "ssss", 1, True)
+            lay_dz_tok(1, 1, "v")
+            lay_x(0, 2, "v")
             quant_dz_tok(1, 1)
-            for i in range(4):
-                if i != 2:
-                    lay_x(1, i, "v")
-                quant_x(0, i)
-                if i == 0:
-                    lay_x(1, 2, "s")
-                open_out1(i)
-                if i < 3:
-                    lay_x(0, i + 1, "v")
-                quant_x(1, i)
-                close_out1(i, "ssss" if i < 3 else "vsvs", 1 if i < 3 else 2)
+            lay_x(1, 2, "v")
+            quant_x(0, 2)
+            quant_x(1, 2)
+            close_out1(2, "ssss", 1, True)
+            lay_x(0, 3, "v")
+            lay_x(1, 3, "v")
+            quant_x(0, 3)
+            quant_x(1, 3)
+            close_out1(3, "svsv", 2, True)

@@ -59,25 +59,21 @@ def tile_implicitrelationencoder_pb_v_kernel(
 
         def load_z(g, lo, hi):
             if lo == 0:
-                z_sb[g] = work.tile([P, PACK, H * DH], F32, name="zt", tag="k16", bufs=6, align_bytes=256)
+                z_sb[g] = work.tile([P, PACK, H * DH], F32, name="zt", tag="k16", bufs=5, align_bytes=256)
             nc.sync.dma_start(out=z_sb[g][:, lo:hi, :], in_=group_view(z_rows, g)[:, lo:hi, :])
 
-        def load_g(g, lo, hi):
-            if lo == 0:
-                g_sb[g] = work.tile([P, PACK, H * DH], BF16, name="gt", tag="k8", bufs=4, align_bytes=256)
-            nc.sync.dma_start(out=g_sb[g][:, lo:hi, :], in_=group_view(g_rows, g)[:, lo:hi, :])
+        def load_g(g):
+            if g == 0:
+                g_sb[0] = work.tile([P, GROUPS, PACK, H * DH], BF16, name="gt", tag="k16", bufs=5, align_bytes=256)
+            nc.sync.dma_start(out=g_sb[0][:, g], in_=group_view(g_rows, g))
 
-        def load_w(h, lo, hi):
-            if lo == 0:
-                w_sb[h] = work.tile([P, 2, PACK * DH], BF16, name="wt", tag="k8", bufs=4, align_bytes=256)
-            nc.sync.dma_start(
-                out=w_sb[h][:, lo:hi, :],
-                in_=out_w[h].rearrange("(c q m) o -> q c (m o)", c=2, m=PACK)[:, lo:hi, :],
-            )
+        def load_w(h):
+            w_sb[h] = work.tile([P, 2, PACK * DH], BF16, name="wt", bufs=2, align_bytes=256)
+            nc.sync.dma_start(out=w_sb[h][:], in_=out_w[h].rearrange("(c q m) o -> q c (m o)", c=2, m=PACK))
 
-        def load_x(g):
-            x_sb[g] = work.tile([P, PACK, H * D], BF16, name="xt", tag="k16", bufs=6, align_bytes=256)
-            nc.sync.dma_start(out=x_sb[g][:], in_=group_view(x_rows, g))
+        def load_x():
+            x_sb[0] = work.tile([P, GROUPS, PACK * H * D], BF16, name="xt", align_bytes=256)
+            nc.sync.dma_start(out=x_sb[0][:], in_=x_rows.rearrange("(g p j) d -> p g (j d)", g=GROUPS, j=PACK))
 
         def make_dz(g, lo, hi):
             dst = dz_sb[g][:].rearrange("p (j h u w e) -> p u j h w e", j=PACK, h=H, u=2, e=2)
@@ -86,7 +82,7 @@ def tile_implicitrelationencoder_pb_v_kernel(
                     out=dst[:, u, lo:hi],
                     in0=z_sb[g][:, lo:hi, :].rearrange("p j (h w u e) -> p u j h w e", h=H, u=2, e=2)[:, u],
                     scalar=0.0,
-                    in1=g_sb[g][:, lo:hi, :].rearrange("p j (h w u e) -> p u j h w e", h=H, u=2, e=2)[:, u],
+                    in1=g_sb[0][:, g, lo:hi, :].rearrange("p j (h w u e) -> p u j h w e", h=H, u=2, e=2)[:, u],
                     op0=GT, op1=MULT,
                 )
 
@@ -160,7 +156,7 @@ def tile_implicitrelationencoder_pb_v_kernel(
         xgrp = {}
 
         def lay_x(g, i, how):
-            xgrp[g, i] = interleave(x_sb[g][:, :, i * CHUNK : (i + 1) * CHUNK], how, 2)
+            xgrp[g, i] = interleave(x_sb[0][:, g, :].rearrange("p (j n) -> p j n", j=PACK)[:, :, i * CHUNK : (i + 1) * CHUNK], how, 2)
 
         def quant_x(g, i):
             nc.vector.quantize_mx(out=xq[:, g * 4 + i, :].bitcast(E4X4), scales=xs[:, g * 4 + i, :], in_=xgrp[g, i][:])
@@ -168,8 +164,11 @@ def tile_implicitrelationencoder_pb_v_kernel(
         o0_sb = {}
 
         def make_out0(g, j, h, cs=(0, 1), engines="ss"):
-            if (g, j // 2) not in o0_sb:
-                o0_sb[g, j // 2] = work.tile([P, 2, H * D], F32, name="o0", tag="k16", bufs=6, align_bytes=256)
+            if (g, j) not in o0_sb:
+                half = work.tile([P, 2, H * D], F32, name="o0", tag="k16", bufs=5, align_bytes=256)
+                for k in range(j, j + 2):
+                    o0_sb[g, k] = (half, j)
+            dst, first = o0_sb[g, j]
             rows = slice(h * P, (h + 1) * P)
             for c in cs:
                 acc = psum.tile([P, CHUNK], F32, name="acc", tag="bank", bufs=8)
@@ -181,12 +180,12 @@ def tile_implicitrelationencoder_pb_v_kernel(
                 )
                 copy_on(
                     engines[c],
-                    out=o0_sb[g, j // 2][:, j % 2, (2 * h + c) * CHUNK : (2 * h + c + 1) * CHUNK], in_=acc[:],
+                    out=dst[:, j - first, (2 * h + c) * CHUNK : (2 * h + c + 1) * CHUNK], in_=acc[:],
                 )
 
         def store_out0(g, lo, hi):
             nc.sync.dma_start(
-                out=group_view(o0_rows, g)[:, lo:hi, :], in_=o0_sb[g, lo // 2][:, lo % 2 : lo % 2 + hi - lo, :]
+                out=group_view(o0_rows, g)[:, lo:hi, :], in_=o0_sb[g, lo][0][:, lo - o0_sb[g, lo][1] : hi - o0_sb[g, lo][1], :]
             )
 
         o1_acc = {}
@@ -207,119 +206,106 @@ def tile_implicitrelationencoder_pb_v_kernel(
             for e in range(4):
                 pass_out1(i, 0, e)
 
-        def close_out1(i, engines, pieces=1, both=False):
+        o1_sb = {}
+
+        def close_out1(i, engines, both=True):
             h, c = divmod(i, 2)
-            o1 = work.tile([P, 4, DH], F32, name="o1", tag="k8", bufs=4, align_bytes=256)
+            if c == 0:
+                o1_sb[h] = work.tile([P, 8, DH], F32, name="o1", tag="k16", bufs=5, align_bytes=256)
             for e in range(4):
                 if both:
                     pass_out1(i, 0, e)
                 pass_out1(i, 1, e)
                 copy_on(
                     engines[e],
-                    out=o1[:, e, :].rearrange("p (w u e) -> p w u e", u=2, e=2),
+                    out=o1_sb[h][:, 4 * c + e, :].rearrange("p (w u e) -> p w u e", u=2, e=2),
                     in_=o1_acc[i, e][:].rearrange("p (u w e) -> p w u e", u=2, e=2),
                 )
-                if (e + 1) % (4 // pieces) == 0:
-                    es = slice((e + 1 - 4 // pieces) // 2, (e + 1) // 2)
-                    nc.sync.dma_start(
-                        out=out_1[h].rearrange("(c a q m) o -> c q a (m o)", c=2, a=2, m=2)[c][:, es, :],
-                        in_=o1[:].rearrange("p (a m) o -> p a (m o)", m=2)[:, es, :],
-                    )
+
+        def store_out1(h, lo, hi):
+            nc.sync.dma_start(
+                out=out_1[h].rearrange("(a q m) o -> q a (m o)", a=4, m=2)[:, lo:hi, :],
+                in_=o1_sb[h][:].rearrange("p (a m) o -> p a (m o)", m=2)[:, lo:hi, :],
+            )
 
         with tc.manual_schedule():
-            load_w(0, 0, 2)
-            load_z(0, 0, 1)
-            load_g(0, 0, 2)
-            load_z(0, 1, 2)
+            load_w(0)
+            load_z(0, 0, 2)
+            load_g(0)
+            load_w(1)
             load_z(0, 2, 4)
-            load_g(0, 2, 4)
-            load_w(1, 0, 2)
-            load_g(1, 0, 4)
+            load_g(1)
             load_z(1, 0, 4)
-            load_x(0)
-            load_x(1)
-            turn_w(0, 0, 0)
-            turn_w(0, 0, 1)
-            turn_w(0, 1, 0)
-            turn_w(0, 1, 1)
-            make_dz(0, 0, 1)
+            load_x()
+            for c in range(2):
+                for mm in range(2):
+                    turn_w(0, c, mm)
             quant_w(0, 0)
+            make_dz(0, 0, 1)
             turn_dz(0, 0)
             make_dz(0, 1, 2)
-            turn_dz(0, 1)
             quant_w(0, 1)
-            quant_dz_feat(0, 0, 1)
-            make_dz(0, 2, 3)
-            make_out0(0, 0, 0)
-            turn_dz(0, 2)
-            quant_dz_feat(0, 1, 2)
-            make_dz(0, 3, 4)
-            make_out0(0, 1, 0)
-            turn_dz(0, 3)
-            quant_dz_feat(0, 2, 3)
+            turn_dz(0, 1)
             turn_w(1, 0, 0)
-            make_out0(0, 2, 0)
-            lay_dz_tok(0, 0, "v")
-            quant_dz_feat(0, 3, 4)
+            quant_dz_feat(0, 0, 1)
+            make_out0(0, 0, 0)
+            quant_dz_feat(0, 1, 2)
             turn_w(1, 0, 1)
+            make_dz(0, 2, 3)
+            make_out0(0, 1, 0)
             turn_w(1, 1, 0)
-            make_out0(0, 3, 0)
-            turn_w(1, 1, 1)
-            lay_dz_tok(0, 1, "v")
-            quant_dz_tok(0, 0)
+            turn_dz(0, 2)
+            make_dz(0, 3, 4)
+            lay_dz_tok(0, 0, "v")
             quant_w(1, 0)
-            quant_dz_tok(0, 1)
-            make_dz(1, 0, 1)
-            quant_w(1, 1)
-            make_dz(1, 1, 2)
+            turn_w(1, 1, 1)
+            turn_dz(0, 3)
             make_out0(0, 0, 1, (0,))
             make_out0(0, 1, 1, (0,))
-            make_out0(0, 2, 1, (0,))
-            turn_dz(1, 0)
+            lay_dz_tok(0, 1, "v")
+            quant_dz_feat(0, 2, 3)
+            quant_dz_tok(0, 0)
+            quant_w(1, 1)
+            quant_dz_feat(0, 3, 4)
+            make_out0(0, 2, 0)
             make_out0(0, 0, 1, (1,))
             make_out0(0, 1, 1, (1,))
             store_out0(0, 0, 2)
+            quant_dz_tok(0, 1)
+            make_dz(1, 0, 2)
+            make_out0(0, 2, 1)
+            make_out0(0, 3, 0)
+            turn_dz(1, 0)
             turn_dz(1, 1)
             make_dz(1, 2, 4)
-            make_out0(0, 2, 1, (1,))
-            make_out0(0, 3, 1, (0,))
+            make_out0(0, 3, 1)
+            store_out0(0, 2, 4)
             lay_dz_tok(1, 0, "v")
             quant_dz_feat(1, 0, 2)
             turn_dz(1, 2)
             turn_dz(1, 3)
-            make_out0(0, 3, 1, (1,))
-            store_out0(0, 2, 4)
+            lay_dz_tok(1, 1, "v")
             quant_dz_tok(1, 0)
-            lay_x(0, 0, "v")
-            quant_dz_feat(1, 2, 4)
             make_out0(1, 0, 0)
             make_out0(1, 0, 1)
+            quant_dz_feat(1, 2, 4)
+            quant_dz_tok(1, 1)
             make_out0(1, 1, 0)
             make_out0(1, 1, 1)
             store_out0(1, 0, 2)
-            lay_x(1, 0, "v")
-            quant_x(0, 0)
-            quant_x(1, 0)
-            make_out0(1, 2, 0, engines="vs")
-            make_out0(1, 2, 1)
-            make_out0(1, 3, 0)
-            make_out0(1, 3, 1)
+            for j in range(2, 4):
+                for h in range(H):
+                    make_out0(1, j, h)
             store_out0(1, 2, 4)
-            close_out1(0, "ssss", 1, True)
-            lay_x(0, 1, "v")
-            lay_x(1, 1, "v")
-            quant_x(0, 1)
-            quant_x(1, 1)
-            close_out1(1, "ssss", 1, True)
-            lay_dz_tok(1, 1, "v")
-            lay_x(0, 2, "v")
-            quant_dz_tok(1, 1)
-            lay_x(1, 2, "v")
-            quant_x(0, 2)
-            quant_x(1, 2)
-            close_out1(2, "ssss", 1, True)
-            lay_x(0, 3, "v")
-            lay_x(1, 3, "v")
-            quant_x(0, 3)
-            quant_x(1, 3)
-            close_out1(3, "svsv", 2, True)
+            for i in range(4):
+                for g in range(GROUPS):
+                    lay_x(g, i, "v")
+                quant_x(0, i)
+                if i == 3:
+                    open_out1(i)
+                quant_x(1, i)
+                close_out1(i, "ssss" if i < 3 else "svsv", i < 3)
+                if i == 1:
+                    store_out1(0, 0, 4)
+                if i > 1:
+                    store_out1(1, 2 * i - 4, 2 * i - 2)

@@ -68,8 +68,8 @@ def tile_implicitrelationencoder_pb_v_kernel(
             nc.sync.dma_start(out=g_sb[0][:, g], in_=group_view(g_rows, g))
 
         def load_w(h):
-            w_sb[h] = work.tile([P, 2, PACK * DH], BF16, name="wt", bufs=2, align_bytes=256)
-            nc.sync.dma_start(out=w_sb[h][:], in_=out_w[h].rearrange("(c q m) o -> q c (m o)", c=2, m=PACK))
+            w_sb[h] = work.tile([P, W_ROWS * DH], BF16, name="wt", bufs=2, align_bytes=256)
+            nc.sync.dma_start(out=w_sb[h][:], in_=out_w[h].rearrange("(q m) o -> q (m o)", m=W_ROWS))
 
         def load_x():
             x_sb[0] = work.tile([P, GROUPS, PACK * H * D], BF16, name="xt", align_bytes=256)
@@ -122,12 +122,12 @@ def tile_implicitrelationencoder_pb_v_kernel(
         def turn_w(h, c, mm):
             if mm == 0:
                 wgrp[h, c] = work.tile([P, 2048], BF16, name="wgrp", tag="wgrp", bufs=3, align_bytes=64)
-            words = w_sb[h][:, c, :].bitcast(F32)
+            words = w_sb[h][:].bitcast(F32)
             dst = wgrp[h, c][:].bitcast(F32).rearrange("p (q k) -> p q k", k=2 * PACK)
             tp = psum.tile([P, 4, P], F32, name="tp", tag="bank", bufs=8)
             for i in range(2):
                 for u in range(2):
-                    off = (2 * mm + i) * 256
+                    off = (PACK * c + 2 * mm + i) * 256
                     nc.tensor.transpose(tp[:, 2 * i + u, :], words[:, off + u : off + 256 : 2], ident[:])
             nc.scalar.copy(out=dst[:, :, 4 * mm : 4 * mm + 4], in_=tp[:].rearrange("p k q -> p q k"))
 
@@ -140,8 +140,8 @@ def tile_implicitrelationencoder_pb_v_kernel(
                 dst = grp[:].rearrange("p (c i j) -> p c j i", i=4, j=PACK)
                 src = src.rearrange("p j (c i) -> p c j i", i=4)
             else:
-                dst = grp[:].rearrange("p (m c s j) -> p c j s m", m=2, s=2, j=PACK)
-                src = src.rearrange("p j (c s m) -> p c j s m", s=2, m=2)
+                dst = grp[:].rearrange("p (m c s j) -> p c j s m", m=PACK, s=2, j=PACK)
+                src = src.rearrange("p j (c s m) -> p c j s m", s=2, m=PACK)
             copy_on(engine, out=dst, in_=src)
             return grp
 
@@ -180,7 +180,8 @@ def tile_implicitrelationencoder_pb_v_kernel(
                 )
                 copy_on(
                     engines[c],
-                    out=dst[:, j - first, (2 * h + c) * CHUNK : (2 * h + c + 1) * CHUNK], in_=acc[:],
+                    out=dst[:, j - first, h * D : (h + 1) * D].rearrange("p (q c m) -> p c q m", c=2, m=PACK)[:, c],
+                    in_=acc[:].rearrange("p (q m) -> p q m", m=PACK),
                 )
 
         def store_out0(g, lo, hi):
@@ -191,8 +192,7 @@ def tile_implicitrelationencoder_pb_v_kernel(
         o1_acc = {}
 
         def pass_out1(i, g, e):
-            a, m = divmod(e, 2)
-            cols = slice((2 * m + a) * P, (2 * m + a + 1) * P)
+            cols = slice(e * P, (e + 1) * P)
             if g == 0:
                 o1_acc[i, e] = psum.tile([P, CHUNK], F32, name="acc", tag="bank", bufs=8)
             nc.tensor.matmul_mx(
@@ -222,10 +222,11 @@ def tile_implicitrelationencoder_pb_v_kernel(
                     in_=o1_acc[i, e][:].rearrange("p (u w e) -> p w u e", u=2, e=2),
                 )
 
-        def store_out1(h, lo, hi):
+        def store_out1(i):
+            h, c = divmod(i, 2)
             nc.sync.dma_start(
-                out=out_1[h].rearrange("(a q m) o -> q a (m o)", a=4, m=2)[:, lo:hi, :],
-                in_=o1_sb[h][:].rearrange("p (a m) o -> p a (m o)", m=2)[:, lo:hi, :],
+                out=out_1[h].rearrange("(c q m) o -> c q (m o)", c=2, m=PACK)[c],
+                in_=o1_sb[h][:].rearrange("p (c m) o -> p c (m o)", c=2)[:, c, :],
             )
 
         with tc.manual_schedule():
@@ -290,7 +291,7 @@ def tile_implicitrelationencoder_pb_v_kernel(
             make_out0(1, 0, 1)
             quant_dz_feat(1, 2, 4)
             quant_dz_tok(1, 1)
-            make_out0(1, 1, 0)
+            make_out0(1, 1, 0, engines="vs")
             make_out0(1, 1, 1)
             store_out0(1, 0, 2)
             for j in range(2, 4):
@@ -305,7 +306,4 @@ def tile_implicitrelationencoder_pb_v_kernel(
                     open_out1(i)
                 quant_x(1, i)
                 close_out1(i, "ssss" if i < 3 else "svsv", i < 3)
-                if i == 1:
-                    store_out1(0, 0, 4)
-                if i > 1:
-                    store_out1(1, 2 * i - 4, 2 * i - 2)
+                store_out1(i)

@@ -134,15 +134,17 @@ def tile_implicitrelationencoder_pb_v_kernel(
         def quant_w(h, c):
             nc.vector.quantize_mx(out=wq[:, 2 * h + c, :].bitcast(E4X4), scales=ws[:, 2 * h + c, :], in_=wgrp[h, c][:])
 
-        def interleave(src, engine, rows):
-            grp = work.tile([P, 2048], BF16, name="grp", tag="il_" + engine, bufs=3 if engine == "v" else 1, align_bytes=64)
+        def interleave(src, engine, rows, grp=None):
+            half = {"s": slice(0, 32), "w": slice(32, 64), "v": slice(0, 64)}[engine]
+            if grp is None:
+                grp = work.tile([P, 2048], BF16, name="grp", tag="il_" + engine, bufs=3 if engine == "v" else 1, align_bytes=64)
             if rows == 1:
                 dst = grp[:].rearrange("p (c i j) -> p c j i", i=4, j=PACK)
                 src = src.rearrange("p j (c i) -> p c j i", i=4)
             else:
-                dst = grp[:].rearrange("p (m c s j) -> p c j s m", m=PACK, s=2, j=PACK)
-                src = src.rearrange("p j (c s m) -> p c j s m", s=2, m=PACK)
-            copy_on(engine, out=dst, in_=src)
+                dst = grp[:].rearrange("p (m c s j) -> p c j s m", m=PACK, s=2, j=PACK)[:, half]
+                src = src.rearrange("p j (c s m) -> p c j s m", s=2, m=PACK)[:, half]
+            copy_on("s" if engine == "s" else "v", out=dst, in_=src)
             return grp
 
         tgrp = {}
@@ -156,33 +158,41 @@ def tile_implicitrelationencoder_pb_v_kernel(
         xgrp = {}
 
         def lay_x(g, i, how):
-            xgrp[g, i] = interleave(x_sb[0][:, g, :].rearrange("p (j n) -> p j n", j=PACK)[:, :, i * CHUNK : (i + 1) * CHUNK], how, 2)
+            xgrp[g, i] = interleave(x_sb[0][:, g, :].rearrange("p (j n) -> p j n", j=PACK)[:, :, i * CHUNK : (i + 1) * CHUNK], how, 2, xgrp.get((g, i)))
 
         def quant_x(g, i):
             nc.vector.quantize_mx(out=xq[:, g * 4 + i, :].bitcast(E4X4), scales=xs[:, g * 4 + i, :], in_=xgrp[g, i][:])
 
         o0_sb = {}
 
-        def make_out0(g, j, h, cs=(0, 1), engines="ss"):
+        o0_acc = {}
+
+        def mul_out0(g, j, h, c):
             if (g, j) not in o0_sb:
                 half = work.tile([P, 2, H * D], F32, name="o0", tag="k16", bufs=5, align_bytes=256)
                 for k in range(j, j + 2):
                     o0_sb[g, k] = (half, j)
-            dst, first = o0_sb[g, j]
             rows = slice(h * P, (h + 1) * P)
+            o0_acc[g, j, h, c] = psum.tile([P, CHUNK], F32, name="acc", tag="bank", bufs=8)
+            nc.tensor.matmul_mx(
+                out=o0_acc[g, j, h, c][:],
+                lhsT=fq[:, PACK * g + j, rows].bitcast(E5X4), lhsT_scale=fs[:, PACK * g + j, rows],
+                rhs=wq[:, 2 * h + c, :].bitcast(E4X4), rhs_scale=ws[:, 2 * h + c, :],
+                start=True, stop=True,
+            )
+
+        def take_out0(g, j, h, c, engine):
+            dst, first = o0_sb[g, j]
+            copy_on(
+                engine,
+                out=dst[:, j - first, h * D : (h + 1) * D].rearrange("p (q c m) -> p c q m", c=2, m=PACK)[:, c],
+                in_=o0_acc[g, j, h, c][:].rearrange("p (q m) -> p q m", m=PACK),
+            )
+
+        def make_out0(g, j, h, cs=(0, 1)):
             for c in cs:
-                acc = psum.tile([P, CHUNK], F32, name="acc", tag="bank", bufs=8)
-                nc.tensor.matmul_mx(
-                    out=acc[:],
-                    lhsT=fq[:, PACK * g + j, rows].bitcast(E5X4), lhsT_scale=fs[:, PACK * g + j, rows],
-                    rhs=wq[:, 2 * h + c, :].bitcast(E4X4), rhs_scale=ws[:, 2 * h + c, :],
-                    start=True, stop=True,
-                )
-                copy_on(
-                    engines[c],
-                    out=dst[:, j - first, h * D : (h + 1) * D].rearrange("p (q c m) -> p c q m", c=2, m=PACK)[:, c],
-                    in_=acc[:].rearrange("p (q m) -> p q m", m=PACK),
-                )
+                mul_out0(g, j, h, c)
+                take_out0(g, j, h, c, "s")
 
         def store_out0(g, lo, hi):
             nc.sync.dma_start(
@@ -231,76 +241,84 @@ def tile_implicitrelationencoder_pb_v_kernel(
 
         with tc.manual_schedule():
             load_w(0)
-            load_z(0, 0, 2)
+            load_z(0, 0, 1)
             load_g(0)
+            load_z(0, 1, 4)
             load_w(1)
-            load_z(0, 2, 4)
             load_g(1)
             load_z(1, 0, 4)
             load_x()
             for c in range(2):
                 for mm in range(2):
                     turn_w(0, c, mm)
-            quant_w(0, 0)
             make_dz(0, 0, 1)
+            quant_w(0, 0)
             turn_dz(0, 0)
-            make_dz(0, 1, 2)
             quant_w(0, 1)
-            turn_dz(0, 1)
-            turn_w(1, 0, 0)
             quant_dz_feat(0, 0, 1)
+            make_dz(0, 1, 2)
             make_out0(0, 0, 0)
-            quant_dz_feat(0, 1, 2)
-            turn_w(1, 0, 1)
+            turn_dz(0, 1)
             make_dz(0, 2, 3)
-            make_out0(0, 1, 0)
-            turn_w(1, 1, 0)
+            turn_w(1, 0, 0)
             turn_dz(0, 2)
             make_dz(0, 3, 4)
-            lay_dz_tok(0, 0, "v")
-            quant_w(1, 0)
-            turn_w(1, 1, 1)
+            quant_dz_feat(0, 1, 2)
+            turn_w(1, 0, 1)
+            make_out0(0, 1, 0)
             turn_dz(0, 3)
+            lay_dz_tok(0, 0, "v")
+            quant_dz_feat(0, 2, 3)
+            turn_w(1, 1, 0)
+            make_out0(0, 2, 0)
+            turn_w(1, 1, 1)
+            quant_w(1, 0)
+            lay_dz_tok(0, 1, "v")
+            quant_dz_feat(0, 3, 4)
+            quant_dz_tok(0, 0)
             make_out0(0, 0, 1, (0,))
             make_out0(0, 1, 1, (0,))
-            lay_dz_tok(0, 1, "v")
-            quant_dz_feat(0, 2, 3)
-            quant_dz_tok(0, 0)
+            make_out0(0, 3, 0)
+            quant_dz_tok(0, 1)
+            make_dz(1, 0, 1)
             quant_w(1, 1)
-            quant_dz_feat(0, 3, 4)
-            make_out0(0, 2, 0)
+            make_dz(1, 1, 2)
             make_out0(0, 0, 1, (1,))
             make_out0(0, 1, 1, (1,))
             store_out0(0, 0, 2)
-            quant_dz_tok(0, 1)
-            make_dz(1, 0, 2)
             make_out0(0, 2, 1)
-            make_out0(0, 3, 0)
             turn_dz(1, 0)
             turn_dz(1, 1)
             make_dz(1, 2, 4)
             make_out0(0, 3, 1)
             store_out0(0, 2, 4)
             lay_dz_tok(1, 0, "v")
-            quant_dz_feat(1, 0, 2)
+            quant_dz_feat(1, 0, 1)
+            lay_dz_tok(1, 1, "v")
             turn_dz(1, 2)
             turn_dz(1, 3)
-            lay_dz_tok(1, 1, "v")
+            quant_dz_feat(1, 1, 2)
             quant_dz_tok(1, 0)
+            quant_dz_tok(1, 1)
             make_out0(1, 0, 0)
             make_out0(1, 0, 1)
             quant_dz_feat(1, 2, 4)
-            quant_dz_tok(1, 1)
-            make_out0(1, 1, 0, engines="vs")
+            lay_x(0, 0, "v")
+            mul_out0(1, 1, 0, 0)
+            mul_out0(1, 1, 0, 1)
             make_out0(1, 1, 1)
+            take_out0(1, 1, 0, 0, "v")
+            take_out0(1, 1, 0, 1, "v")
             store_out0(1, 0, 2)
-            for j in range(2, 4):
+            for j in range(2, PACK):
                 for h in range(H):
                     make_out0(1, j, h)
             store_out0(1, 2, 4)
+            lay_x(1, 3, "s")
             for i in range(4):
                 for g in range(GROUPS):
-                    lay_x(g, i, "v")
+                    if (g, i) != (0, 0):
+                        lay_x(g, i, "w" if (g, i) == (1, 3) else "v")
                 quant_x(0, i)
                 if i == 3:
                     open_out1(i)

@@ -12,7 +12,7 @@ PACK = 4
 GROUP = P * PACK
 GROUPS = T // GROUP
 CHUNK = 512
-W_ROWS = D // P
+W_SLOTS = H * D // P
 
 F32 = mybir.dt.float32
 BF16 = mybir.dt.bfloat16
@@ -59,17 +59,17 @@ def tile_implicitrelationencoder_pb_v_kernel(
 
         def load_z(g, lo, hi):
             if lo == 0:
-                z_sb[g] = work.tile([P, PACK, H * DH], F32, name="zt", tag="k16", bufs=5, align_bytes=256)
+                z_sb[g] = work.tile([P, PACK, H * DH], F32, name="zt", tag="k16", bufs=6, align_bytes=256)
             nc.sync.dma_start(out=z_sb[g][:, lo:hi, :], in_=group_view(z_rows, g)[:, lo:hi, :])
 
         def load_g(g):
             if g == 0:
-                g_sb[0] = work.tile([P, GROUPS, PACK, H * DH], BF16, name="gt", tag="k16", bufs=5, align_bytes=256)
+                g_sb[0] = work.tile([P, GROUPS, PACK, H * DH], BF16, name="gt", tag="k16", bufs=6, align_bytes=256)
             nc.sync.dma_start(out=g_sb[0][:, g], in_=group_view(g_rows, g))
 
-        def load_w(h):
-            w_sb[h] = work.tile([P, W_ROWS * DH], BF16, name="wt", bufs=2, align_bytes=256)
-            nc.sync.dma_start(out=w_sb[h][:], in_=out_w[h].rearrange("(q m) o -> q (m o)", m=W_ROWS))
+        def load_w():
+            w_sb[0] = work.tile([P, W_SLOTS * DH], BF16, name="wt", tag="k16", bufs=6, align_bytes=256)
+            nc.sync.dma_start(out=w_sb[0][:], in_=out_w.rearrange("h (q m) o -> (h q) (m o)", m=W_SLOTS))
 
         def load_x():
             x_sb[0] = work.tile([P, GROUPS, PACK * H * D], BF16, name="xt", align_bytes=256)
@@ -119,20 +119,29 @@ def tile_implicitrelationencoder_pb_v_kernel(
 
         wgrp = {}
 
-        def turn_w(h, c, mm):
-            if mm == 0:
-                wgrp[h, c] = work.tile([P, 2048], BF16, name="wgrp", tag="wgrp", bufs=3, align_bytes=64)
-            words = w_sb[h][:].bitcast(F32)
-            dst = wgrp[h, c][:].bitcast(F32).rearrange("p (q k) -> p q k", k=2 * PACK)
+        def sort_w(lo, hi):
+            if lo == 0:
+                w_sb[1] = work.tile([P, W_SLOTS * DH], BF16, name="wsort", tag="k16", bufs=6, align_bytes=256)
+            nc.vector.tensor_copy(
+                out=w_sb[1][:].rearrange("p (m u w e) -> p m u w e", m=W_SLOTS, u=2, e=2)[:, lo:hi],
+                in_=w_sb[0][:].rearrange("p (m w u e) -> p m u w e", m=W_SLOTS, u=2, e=2)[:, lo:hi],
+            )
+
+        def turn_w(c, k):
+            if k == 0:
+                wgrp[c] = work.tile([P, 4096], BF16, name="wgrp", tag="wgrp", bufs=2, align_bytes=64)
+            words = w_sb[1][:].bitcast(F32)
+            dst = wgrp[c][:].bitcast(F32).rearrange("p (q n) -> p q n", n=W_SLOTS)
             tp = psum.tile([P, 4, P], F32, name="tp", tag="bank", bufs=8)
-            for i in range(2):
-                for u in range(2):
-                    off = (PACK * c + 2 * mm + i) * 256
-                    nc.tensor.transpose(tp[:, 2 * i + u, :], words[:, off + u : off + 256 : 2], ident[:])
-            nc.scalar.copy(out=dst[:, :, 4 * mm : 4 * mm + 4], in_=tp[:].rearrange("p k q -> p q k"))
+            for n in range(4):
+                off = (16 * c + 4 * k + n) * P
+                nc.tensor.transpose(tp[:, n, :], words[:, off : off + P], ident[:])
+            nc.scalar.copy(out=dst[:, :, 4 * k : 4 * k + 4], in_=tp[:].rearrange("p n q -> p q n"))
 
         def quant_w(h, c):
-            nc.vector.quantize_mx(out=wq[:, 2 * h + c, :].bitcast(E4X4), scales=ws[:, 2 * h + c, :], in_=wgrp[h, c][:])
+            nc.vector.quantize_mx(
+                out=wq[:, 2 * h + c, :].bitcast(E4X4), scales=ws[:, 2 * h + c, :], in_=wgrp[c][:, h * 2048 : (h + 1) * 2048]
+            )
 
         def interleave(src, engine, rows, grp=None):
             half = {"s": slice(0, 32), "w": slice(32, 64), "v": slice(0, 64)}[engine]
@@ -169,7 +178,7 @@ def tile_implicitrelationencoder_pb_v_kernel(
 
         def mul_out0(g, j, h, c):
             if (g, j) not in o0_sb:
-                half = work.tile([P, 2, H * D], F32, name="o0", tag="k16", bufs=5, align_bytes=256)
+                half = work.tile([P, 2, H * D], F32, name="o0", tag="k16", bufs=6, align_bytes=256)
                 for k in range(j, j + 2):
                     o0_sb[g, k] = (half, j)
             rows = slice(h * P, (h + 1) * P)
@@ -185,8 +194,8 @@ def tile_implicitrelationencoder_pb_v_kernel(
             dst, first = o0_sb[g, j]
             copy_on(
                 engine,
-                out=dst[:, j - first, h * D : (h + 1) * D].rearrange("p (q c m) -> p c q m", c=2, m=PACK)[:, c],
-                in_=o0_acc[g, j, h, c][:].rearrange("p (q m) -> p q m", m=PACK),
+                out=dst[:, j - first, h * D : (h + 1) * D].rearrange("p (q c m) -> p c q m", c=2, m=8)[:, c],
+                in_=o0_acc[g, j, h, c][:].rearrange("p (q m) -> p q m", m=8),
             )
 
         def make_out0(g, j, h, cs=(0, 1)):
@@ -221,7 +230,7 @@ def tile_implicitrelationencoder_pb_v_kernel(
         def close_out1(i, engines, both=True):
             h, c = divmod(i, 2)
             if c == 0:
-                o1_sb[h] = work.tile([P, 8, DH], F32, name="o1", tag="k16", bufs=5, align_bytes=256)
+                o1_sb[h] = work.tile([P, 8, DH], F32, name="o1", tag="k16", bufs=6, align_bytes=256)
             for e in range(4):
                 if both:
                     pass_out1(i, 0, e)
@@ -240,81 +249,79 @@ def tile_implicitrelationencoder_pb_v_kernel(
             )
 
         with tc.manual_schedule():
-            load_w(0)
+            load_w()
             load_z(0, 0, 1)
             load_g(0)
             load_z(0, 1, 4)
-            load_w(1)
             load_g(1)
             load_z(1, 0, 4)
             load_x()
             for c in range(2):
-                for mm in range(2):
-                    turn_w(0, c, mm)
+                for half in range(2):
+                    sort_w(8 * c + 4 * half, 8 * c + 4 * half + 4)
+            for k in range(4):
+                turn_w(0, k)
             make_dz(0, 0, 1)
-            quant_w(0, 0)
+            turn_w(1, 0)
+            turn_w(1, 1)
             turn_dz(0, 0)
-            quant_w(0, 1)
+            turn_w(1, 2)
+            turn_w(1, 3)
+            quant_w(0, 0)
+            quant_w(1, 0)
             quant_dz_feat(0, 0, 1)
             make_dz(0, 1, 2)
-            make_out0(0, 0, 0)
+            make_out0(0, 0, 0, (0,))
+            make_out0(0, 0, 1, (0,))
             turn_dz(0, 1)
+            quant_w(0, 1)
+            quant_w(1, 1)
             make_dz(0, 2, 3)
-            turn_w(1, 0, 0)
+            make_out0(0, 0, 0, (1,))
+            make_out0(0, 0, 1, (1,))
             turn_dz(0, 2)
-            make_dz(0, 3, 4)
             quant_dz_feat(0, 1, 2)
-            turn_w(1, 0, 1)
+            make_dz(0, 3, 4)
             make_out0(0, 1, 0)
             turn_dz(0, 3)
+            make_out0(0, 1, 1)
+            store_out0(0, 0, 2)
             lay_dz_tok(0, 0, "v")
             quant_dz_feat(0, 2, 3)
-            turn_w(1, 1, 0)
-            make_out0(0, 2, 0)
-            turn_w(1, 1, 1)
-            quant_w(1, 0)
-            lay_dz_tok(0, 1, "v")
+            make_dz(1, 0, 1)
             quant_dz_feat(0, 3, 4)
             quant_dz_tok(0, 0)
-            make_out0(0, 0, 1, (0,))
-            make_out0(0, 1, 1, (0,))
-            make_out0(0, 3, 0)
-            quant_dz_tok(0, 1)
-            make_dz(1, 0, 1)
-            quant_w(1, 1)
             make_dz(1, 1, 2)
-            make_out0(0, 0, 1, (1,))
-            make_out0(0, 1, 1, (1,))
-            store_out0(0, 0, 2)
+            make_out0(0, 2, 0)
             make_out0(0, 2, 1)
+            make_out0(0, 3, 0)
             turn_dz(1, 0)
             turn_dz(1, 1)
             make_dz(1, 2, 4)
             make_out0(0, 3, 1)
             store_out0(0, 2, 4)
-            lay_dz_tok(1, 0, "v")
+            lay_dz_tok(0, 1, "v")
             quant_dz_feat(1, 0, 1)
+            lay_dz_tok(1, 0, "v")
+            quant_dz_tok(0, 1)
+            quant_dz_feat(1, 1, 2)
             lay_dz_tok(1, 1, "v")
             turn_dz(1, 2)
             turn_dz(1, 3)
-            quant_dz_feat(1, 1, 2)
             quant_dz_tok(1, 0)
             quant_dz_tok(1, 1)
             make_out0(1, 0, 0)
             make_out0(1, 0, 1)
             quant_dz_feat(1, 2, 4)
             lay_x(0, 0, "v")
-            mul_out0(1, 1, 0, 0)
-            mul_out0(1, 1, 0, 1)
+            make_out0(1, 1, 0, (0,))
+            make_out0(1, 1, 0, (1,))
             make_out0(1, 1, 1)
-            take_out0(1, 1, 0, 0, "v")
-            take_out0(1, 1, 0, 1, "v")
             store_out0(1, 0, 2)
             for j in range(2, PACK):
                 for h in range(H):
                     make_out0(1, j, h)
             store_out0(1, 2, 4)
-            lay_x(1, 3, "s")
             for i in range(4):
                 for g in range(GROUPS):
                     if (g, i) != (0, 0):
@@ -325,3 +332,5 @@ def tile_implicitrelationencoder_pb_v_kernel(
                 quant_x(1, i)
                 close_out1(i, "ssss" if i < 3 else "svsv", i < 3)
                 store_out1(i)
+                if i == 0:
+                    lay_x(1, 3, "s")

@@ -1,7 +1,6 @@
 from contextlib import ExitStack
 
 import concourse.mybir as mybir
-from concourse.masks import make_identity
 
 T, H, D, DH = 1024, 2, 1024, 512
 FLOPS = 4 * T * H * D * DH
@@ -22,6 +21,8 @@ E4X4 = mybir.dt.float8_e4m3fn_x4
 E5X4 = mybir.dt.float8_e5m2_x4
 GT = mybir.AluOpType.is_gt
 MULT = mybir.AluOpType.mult
+ADD = mybir.AluOpType.add
+EQ = mybir.AluOpType.is_equal
 
 
 def tile_implicitrelationencoder_pb_v_kernel(
@@ -42,7 +43,17 @@ def tile_implicitrelationencoder_pb_v_kernel(
         psum = ctx.enter_context(tc.psum_pool(name="psum", bufs=1))
 
         ident = keep.tile([P, P], F32, name="ident")
-        make_identity(nc, ident[:])
+
+        def build_identity():
+            ones = keep.tile([P, 32], F32, name="ones", align_bytes=64)
+            col = keep.tile([P, 32], F32, name="col", align_bytes=64)
+            row = keep.tile([P, 32], F32, name="row", align_bytes=64)
+            nc.vector.memset(ones[:], 1.0)
+            nc.vector.memset(ident[:], 0.0)
+            nc.vector.tensor_tensor_scan(out=col[:], data0=ones[:], data1=ones[:], initial=0.0, op0=MULT, op1=ADD)
+            nc.vector.transpose(out=row[:], in_=col[:])
+            for q in range(0, P, 32):
+                nc.vector.tensor_tensor(out=ident[q : q + 32, q : q + 32], in0=col[q : q + 32, :], in1=row[q : q + 32, :], op=EQ)
 
         xq = keep.tile([P, GROUPS * H * 2, CHUNK], U32, name="xq", align_bytes=64)
         xs = keep.tile([P, GROUPS * H * 2, CHUNK], U8, name="xs", align_bytes=64)
@@ -256,6 +267,7 @@ def tile_implicitrelationencoder_pb_v_kernel(
             load_g(1)
             load_z(1, 0, 4)
             load_x()
+            build_identity()
             for c in range(2):
                 for half in range(2):
                     sort_w(8 * c + 4 * half, 8 * c + 4 * half + 4)

@@ -10,8 +10,11 @@ P = 128
 PACK = 4
 GROUP = P * PACK
 GROUPS = T // GROUP
-CHUNK = 512
-W_SLOTS = H * D // P
+BANK = 512
+W_ROWS = 8
+X_BLOCKS = D // P
+KIB = 1024
+LAID = {"v": 3, "s": 2}
 
 F32 = mybir.dt.float32
 BF16 = mybir.dt.bfloat16
@@ -29,19 +32,44 @@ def tile_implicitrelationencoder_pb_v_kernel(
     tc, out_t, out_w, out_b, self_feat, vis, z, grad_out, out_0, out_1
 ):
     nc = tc.nc
-    x_rows = out_t.rearrange("b n h d -> (b n) (h d)")
-    z_rows = z.rearrange("b n d -> (b n) d")
-    g_rows = grad_out.rearrange("b n d -> (b n) d")
-    o0_rows = out_0.rearrange("b n h d -> (b n) (h d)")
 
-    def group_view(rows, g):
-        return rows[g * GROUP : (g + 1) * GROUP, :].rearrange("(p j) d -> p j d", j=PACK)
+    def by_group(rows):
+        return rows.rearrange("(g p j) d -> g p j d", g=GROUPS, j=PACK)
+
+    x_hbm = by_group(out_t.rearrange("b n h d -> (b n) (h d)"))
+    z_hbm = by_group(z.rearrange("b n d -> (b n) d"))
+    g_hbm = by_group(grad_out.rearrange("b n d -> (b n) d"))
+    o0_hbm = by_group(out_0.rearrange("b n h d -> (b n) (h d)"))
+    w_hbm = out_w.rearrange("h (q c m) o -> c (h q) (m o)", c=2, m=W_ROWS)
+    o1_hbm = out_1.rearrange("h (q m) o -> h q m o", m=X_BLOCKS)
 
     with ExitStack() as ctx:
         keep = ctx.enter_context(tc.tile_pool(name="keep", bufs=1))
-        work = ctx.enter_context(tc.tile_pool(name="work", bufs=1))
+        arena = ctx.enter_context(tc.tile_pool(name="arena", bufs=1))
         psum = ctx.enter_context(tc.psum_pool(name="psum", bufs=1))
 
+        def placed(name, shape, dtype, at):
+            return arena.tile(shape, dtype, name=name, offset=at * KIB, align_bytes=256)
+
+        def next_bank(shape):
+            return psum.tile(shape, F32, name="bank", tag="bank", bufs=8)
+
+        def copy_on(engine, out, in_):
+            if engine == "v":
+                nc.vector.tensor_copy(out=out, in_=in_)
+            else:
+                nc.scalar.copy(out=out, in_=in_)
+
+        def operand(name, rows, cols):
+            codes = keep.tile([P, rows, cols], U32, name=name + "_codes", align_bytes=64)
+            scales = keep.tile([P, rows, cols], U8, name=name + "_scales", align_bytes=64)
+            return codes, scales
+
+        w_codes, w_scales = operand("w", 2, H * BANK)
+        f_codes, f_scales = operand("f", GROUPS * PACK, H * P)
+        t_codes, t_scales = operand("t", GROUPS * H, DH)
+        x_codes, x_scales = operand("x", GROUPS * 2 * H, BANK)
+        dz = [keep.tile([P, PACK * H * DH], BF16, name="dz%d" % g, align_bytes=64) for g in range(GROUPS)]
         ident = keep.tile([P, P], F32, name="ident")
 
         def build_identity():
@@ -53,296 +81,276 @@ def tile_implicitrelationencoder_pb_v_kernel(
             nc.vector.tensor_tensor_scan(out=col[:], data0=ones[:], data1=ones[:], initial=0.0, op0=MULT, op1=ADD)
             nc.vector.transpose(out=row[:], in_=col[:])
             for q in range(0, P, 32):
-                nc.vector.tensor_tensor(out=ident[q : q + 32, q : q + 32], in0=col[q : q + 32, :], in1=row[q : q + 32, :], op=EQ)
-
-        xq = keep.tile([P, GROUPS * H * 2, CHUNK], U32, name="xq", align_bytes=64)
-        xs = keep.tile([P, GROUPS * H * 2, CHUNK], U8, name="xs", align_bytes=64)
-        tq = keep.tile([P, GROUPS * H, CHUNK], U32, name="tq", align_bytes=64)
-        ts = keep.tile([P, GROUPS * H, CHUNK], U8, name="ts", align_bytes=64)
-        fq = keep.tile([P, GROUPS * PACK, H * P], U32, name="fq", align_bytes=64)
-        fs = keep.tile([P, GROUPS * PACK, H * P], U8, name="fs", align_bytes=64)
-        wq = keep.tile([P, H * 2, CHUNK], U32, name="wq", align_bytes=64)
-        ws = keep.tile([P, H * 2, CHUNK], U8, name="ws", align_bytes=64)
-
-        z_sb, g_sb, w_sb, x_sb, dz_sb = {}, {}, {}, {}, {}
-        for g in range(GROUPS):
-            dz_sb[g] = keep.tile([P, PACK * H * DH], BF16, name="dz%d" % g, align_bytes=64)
-
-        def load_z(g, lo, hi):
-            if lo == 0:
-                z_sb[g] = work.tile([P, PACK, H * DH], F32, name="zt", tag="k16", bufs=6, align_bytes=256)
-            nc.sync.dma_start(out=z_sb[g][:, lo:hi, :], in_=group_view(z_rows, g)[:, lo:hi, :])
-
-        def load_g(g):
-            if g == 0:
-                g_sb[0] = work.tile([P, GROUPS, PACK, H * DH], BF16, name="gt", tag="k16", bufs=6, align_bytes=256)
-            nc.sync.dma_start(out=g_sb[0][:, g], in_=group_view(g_rows, g))
-
-        def load_w():
-            w_sb[0] = work.tile([P, W_SLOTS * DH], BF16, name="wt", tag="k16", bufs=6, align_bytes=256)
-            nc.sync.dma_start(out=w_sb[0][:], in_=out_w.rearrange("h (q m) o -> (h q) (m o)", m=W_SLOTS))
-
-        def load_x():
-            x_sb[0] = work.tile([P, GROUPS, PACK * H * D], BF16, name="xt", align_bytes=256)
-            nc.sync.dma_start(out=x_sb[0][:], in_=x_rows.rearrange("(g p j) d -> p g (j d)", g=GROUPS, j=PACK))
-
-        def make_dz(g, lo, hi):
-            dst = dz_sb[g][:].rearrange("p (j h u w e) -> p u j h w e", j=PACK, h=H, u=2, e=2)
-            for u in range(2):
-                nc.vector.scalar_tensor_tensor(
-                    out=dst[:, u, lo:hi],
-                    in0=z_sb[g][:, lo:hi, :].rearrange("p j (h w u e) -> p u j h w e", h=H, u=2, e=2)[:, u],
-                    scalar=0.0,
-                    in1=g_sb[0][:, g, lo:hi, :].rearrange("p j (h w u e) -> p u j h w e", h=H, u=2, e=2)[:, u],
-                    op0=GT, op1=MULT,
+                nc.vector.tensor_tensor(
+                    out=ident[q : q + 32, q : q + 32], in0=col[q : q + 32, :], in1=row[q : q + 32, :], op=EQ
                 )
 
-        def copy_on(engine, out, in_):
-            if engine == "v":
-                nc.vector.tensor_copy(out=out, in_=in_)
-            else:
-                nc.scalar.copy(out=out, in_=in_)
+        w_raw, w_sorted, w_turned, x_sb, z_sb, g_sb = {}, {}, {}, {}, {}, {}
 
-        fgrp = {}
+        def load_w(c):
+            w_raw[c] = placed("w_raw%d" % c, [P, W_ROWS * DH], BF16, 8 * c)
+            nc.sync.dma_start(out=w_raw[c][:], in_=w_hbm[c])
 
-        def turn_dz(g, j):
-            if j % 2 == 0:
-                fgrp[g, j // 2] = work.tile([P, 2048], BF16, name="fgrp", tag="grp", bufs=3, align_bytes=64)
-            words = dz_sb[g][:].bitcast(F32)
-            tp = psum.tile([P, 4, P], F32, name="tp", tag="bank", bufs=8)
-            for k in range(4):
-                off = (4 * j + k) * P
-                nc.tensor.transpose(tp[:, k, :], words[:, off : off + P], ident[:])
-            nc.scalar.copy(
-                out=fgrp[g, j // 2][:].bitcast(F32)[:, (j % 2) * 512 : (j % 2 + 1) * 512].rearrange(
-                    "p (h r u) -> p h r u", h=H, u=2
-                ),
-                in_=tp[:].rearrange("p (h u) r -> p h r u", u=2),
-            )
+        def load_x(g):
+            x_sb[g] = placed("x%d" % g, [P, PACK, H * D], BF16, 64 + 32 * g)
+            nc.sync.dma_start(out=x_sb[g][:], in_=x_hbm[g])
 
-        def quant_dz_feat(g, lo, hi):
-            rows = slice(PACK * g + lo, PACK * g + hi)
-            nc.vector.quantize_mx(
-                out=fq[:, rows, :].rearrange("p j n -> p (j n)").bitcast(E5X4),
-                scales=fs[:, rows, :].rearrange("p j n -> p (j n)"),
-                in_=fgrp[g, lo // 2][:, (lo % 2) * 1024 : (lo % 2 + hi - lo) * 1024],
-            )
+        def load_g(g):
+            g_sb[g] = placed("g%d" % g, [P, PACK, H * DH], BF16, 112 + 8 * g)
+            nc.sync.dma_start(out=g_sb[g][:], in_=g_hbm[g])
 
-        wgrp = {}
+        def load_z(g, lo, hi):
+            rows = placed("z%d_%d" % (g, lo), [P, hi - lo, H * DH], F32, 48 + 32 * g + 4 * lo)
+            nc.sync.dma_start(out=rows[:], in_=z_hbm[g][:, lo:hi, :])
+            for j in range(lo, hi):
+                z_sb[g, j] = (rows, lo)
 
-        def sort_w(lo, hi):
+        def sort_w(c, lo, hi):
             if lo == 0:
-                w_sb[1] = work.tile([P, W_SLOTS * DH], BF16, name="wsort", tag="k16", bufs=6, align_bytes=256)
+                w_sorted[c] = placed("w_sorted%d" % c, [P, W_ROWS * DH], BF16, 16 + 8 * c)
             nc.vector.tensor_copy(
-                out=w_sb[1][:].rearrange("p (m u w e) -> p m u w e", m=W_SLOTS, u=2, e=2)[:, lo:hi],
-                in_=w_sb[0][:].rearrange("p (m w u e) -> p m u w e", m=W_SLOTS, u=2, e=2)[:, lo:hi],
+                out=w_sorted[c][:].rearrange("p (m u w e) -> p m u w e", m=W_ROWS, u=2, e=2)[:, lo:hi],
+                in_=w_raw[c][:].rearrange("p (m w u e) -> p m u w e", m=W_ROWS, u=2, e=2)[:, lo:hi],
             )
 
-        def turn_w(c, k):
+        def turn_w(c, k, engine):
             if k == 0:
-                wgrp[c] = work.tile([P, 4096], BF16, name="wgrp", tag="wgrp", bufs=2, align_bytes=64)
-            words = w_sb[1][:].bitcast(F32)
-            dst = wgrp[c][:].bitcast(F32).rearrange("p (q n) -> p q n", n=W_SLOTS)
-            tp = psum.tile([P, 4, P], F32, name="tp", tag="bank", bufs=8)
+                w_turned[c] = placed("w_turned%d" % c, [P, P * W_ROWS * PACK], BF16, 32 + 8 * c)
+            words = w_sorted[c][:].bitcast(F32)
+            bank = next_bank([P, 4, P])
             for n in range(4):
-                off = (16 * c + 4 * k + n) * P
-                nc.tensor.transpose(tp[:, n, :], words[:, off : off + P], ident[:])
-            nc.scalar.copy(out=dst[:, :, 4 * k : 4 * k + 4], in_=tp[:].rearrange("p n q -> p q n"))
+                nc.tensor.transpose(bank[:, n, :], words[:, (4 * k + n) * P : (4 * k + n + 1) * P], ident[:])
+            dst = w_turned[c][:].bitcast(F32).rearrange("p (h k q n) -> p k h q n", h=H, k=4, n=4)
+            copy_on(engine, out=dst[:, k], in_=bank[:].rearrange("p n (h q) -> p h q n", h=H))
 
-        def quant_w(h, c):
-            nc.vector.quantize_mx(
-                out=wq[:, 2 * h + c, :].bitcast(E4X4), scales=ws[:, 2 * h + c, :], in_=wgrp[c][:, h * 2048 : (h + 1) * 2048]
+        def quant_w(c):
+            nc.vector.quantize_mx(out=w_codes[:, c, :].bitcast(E4X4), scales=w_scales[:, c, :], in_=w_turned[c][:])
+
+        def make_dz(g, lo, hi):
+            rows, first = z_sb[g, lo]
+            dst = dz[g][:].rearrange("p (j h u w e) -> p u j h w e", j=PACK, h=H, u=2, e=2)[:, :, lo:hi]
+            pre = rows[:, lo - first : hi - first, :].rearrange("p j (h w u e) -> p u j h w e", h=H, u=2, e=2)
+            grad = g_sb[g][:, lo:hi, :].rearrange("p j (h w u e) -> p u j h w e", h=H, u=2, e=2)
+            for u in range(2):
+                nc.vector.scalar_tensor_tensor(
+                    out=dst[:, u], in0=pre[:, u], scalar=0.0, in1=grad[:, u], op0=GT, op1=MULT
+                )
+
+        dz_turned = {}
+
+        def turn_dz(g, j, engine="s"):
+            dz_turned[g, j] = keep.tile([P, H * P * PACK], BF16, name="dz_turned", tag="dz_turned", bufs=4, align_bytes=64)
+            words = dz[g][:].bitcast(F32)
+            bank = next_bank([P, 4, P])
+            for n in range(4):
+                nc.tensor.transpose(bank[:, n, :], words[:, (4 * j + n) * P : (4 * j + n + 1) * P], ident[:])
+            copy_on(
+                engine,
+                out=dz_turned[g, j][:].bitcast(F32).rearrange("p (h r u) -> p h r u", h=H, u=2),
+                in_=bank[:].rearrange("p (h u) r -> p h r u", u=2),
             )
 
-        def interleave(src, engine, rows, grp=None):
-            half = {"s": slice(0, 32), "w": slice(32, 64), "v": slice(0, 64)}[engine]
-            if grp is None:
-                grp = work.tile([P, 2048], BF16, name="grp", tag="il_" + engine, bufs=3 if engine == "v" else 1, align_bytes=64)
-            if rows == 1:
-                dst = grp[:].rearrange("p (c i j) -> p c j i", i=4, j=PACK)
-                src = src.rearrange("p j (c i) -> p c j i", i=4)
-            else:
-                dst = grp[:].rearrange("p (m c s j) -> p c j s m", m=PACK, s=2, j=PACK)[:, half]
-                src = src.rearrange("p j (c s m) -> p c j s m", s=2, m=PACK)[:, half]
-            copy_on("s" if engine == "s" else "v", out=dst, in_=src)
-            return grp
+        def quant_f(g, j):
+            row = PACK * g + j
+            nc.vector.quantize_mx(out=f_codes[:, row, :].bitcast(E5X4), scales=f_scales[:, row, :], in_=dz_turned[g, j][:])
 
-        tgrp = {}
+        def laid_tile(engine):
+            return keep.tile([P, BANK * PACK], BF16, name="laid", tag="laid_" + engine, bufs=LAID[engine], align_bytes=64)
 
-        def lay_dz_tok(g, h, how):
-            tgrp[g, h] = interleave(dz_sb[g][:].rearrange("p (j n) -> p j n", j=PACK)[:, :, h * DH : (h + 1) * DH], how, 1)
+        t_laid, x_laid = {}, {}
 
-        def quant_dz_tok(g, h):
-            nc.vector.quantize_mx(out=tq[:, g * H + h, :].bitcast(E5X4), scales=ts[:, g * H + h, :], in_=tgrp[g, h][:])
+        def lay_t(g, h):
+            t_laid[g, h] = laid_tile("v")
+            nc.vector.tensor_copy(
+                out=t_laid[g, h][:].rearrange("p (c i j) -> p c j i", i=4, j=PACK),
+                in_=dz[g][:].rearrange("p (j h c i) -> p h c j i", j=PACK, h=H, i=4)[:, h],
+            )
 
-        xgrp = {}
+        def quant_t(g, h):
+            row = g * H + h
+            nc.vector.quantize_mx(out=t_codes[:, row, :].bitcast(E5X4), scales=t_scales[:, row, :], in_=t_laid[g, h][:])
 
-        def lay_x(g, i, how):
-            xgrp[g, i] = interleave(x_sb[0][:, g, :].rearrange("p (j n) -> p j n", j=PACK)[:, :, i * CHUNK : (i + 1) * CHUNK], how, 2, xgrp.get((g, i)))
+        def lay_x(g, i, engine, lo=0, hi=P):
+            h, c = divmod(i, 2)
+            if lo == 0:
+                x_laid[g, i] = laid_tile(engine)
+            src = x_sb[g][:, :, h * D : (h + 1) * D].rearrange("p j (q c m) -> p c q j m", c=2, m=4)[:, c]
+            dst = x_laid[g, i][:].rearrange("p (m q j) -> p q j m", m=4, j=PACK)
+            copy_on(engine, out=dst[:, lo:hi], in_=src[:, lo:hi])
 
         def quant_x(g, i):
-            nc.vector.quantize_mx(out=xq[:, g * 4 + i, :].bitcast(E4X4), scales=xs[:, g * 4 + i, :], in_=xgrp[g, i][:])
+            row = 2 * H * g + i
+            nc.vector.quantize_mx(out=x_codes[:, row, :].bitcast(E4X4), scales=x_scales[:, row, :], in_=x_laid[g, i][:])
 
-        o0_sb = {}
-
-        o0_acc = {}
+        o0_sb, o1_sb, o0_acc, o1_acc = {}, {}, {}, {}
 
         def mul_out0(g, j, h, c):
-            if (g, j) not in o0_sb:
-                half = work.tile([P, 2, H * D], F32, name="o0", tag="k16", bufs=6, align_bytes=256)
-                for k in range(j, j + 2):
-                    o0_sb[g, k] = (half, j)
-            rows = slice(h * P, (h + 1) * P)
-            o0_acc[g, j, h, c] = psum.tile([P, CHUNK], F32, name="acc", tag="bank", bufs=8)
+            o0_acc[g, j, h, c] = next_bank([P, BANK])
             nc.tensor.matmul_mx(
                 out=o0_acc[g, j, h, c][:],
-                lhsT=fq[:, PACK * g + j, rows].bitcast(E5X4), lhsT_scale=fs[:, PACK * g + j, rows],
-                rhs=wq[:, 2 * h + c, :].bitcast(E4X4), rhs_scale=ws[:, 2 * h + c, :],
+                lhsT=f_codes[:, PACK * g + j, h * P : (h + 1) * P].bitcast(E5X4),
+                lhsT_scale=f_scales[:, PACK * g + j, h * P : (h + 1) * P],
+                rhs=w_codes[:, c, h * BANK : (h + 1) * BANK].bitcast(E4X4),
+                rhs_scale=w_scales[:, c, h * BANK : (h + 1) * BANK],
                 start=True, stop=True,
             )
 
         def take_out0(g, j, h, c, engine):
-            dst, first = o0_sb[g, j]
+            if g not in o0_sb:
+                o0_sb[g] = placed("o0_%d" % g, [P, PACK, H * D], F32, 32 * g)
             copy_on(
                 engine,
-                out=dst[:, j - first, h * D : (h + 1) * D].rearrange("p (q c m) -> p c q m", c=2, m=8)[:, c],
-                in_=o0_acc[g, j, h, c][:].rearrange("p (q m) -> p q m", m=8),
+                out=o0_sb[g][:, j, h * D : (h + 1) * D].rearrange("p (q c k s) -> p c q k s", c=2, k=4, s=2)[:, c],
+                in_=o0_acc[g, j, h, c][:].rearrange("p (k q s) -> p q k s", k=4, s=2),
             )
 
-        def make_out0(g, j, h, cs=(0, 1)):
-            for c in cs:
-                mul_out0(g, j, h, c)
-                take_out0(g, j, h, c, "s")
+        def out0_bank(g, j, h, c, engine="s"):
+            mul_out0(g, j, h, c)
+            take_out0(g, j, h, c, engine)
+
+        def out0(g, j, h, engine="s"):
+            for c in range(2):
+                out0_bank(g, j, h, c, engine)
 
         def store_out0(g, lo, hi):
-            nc.sync.dma_start(
-                out=group_view(o0_rows, g)[:, lo:hi, :], in_=o0_sb[g, lo][0][:, lo - o0_sb[g, lo][1] : hi - o0_sb[g, lo][1], :]
-            )
+            nc.sync.dma_start(out=o0_hbm[g][:, lo:hi, :], in_=o0_sb[g][:, lo:hi, :])
 
-        o1_acc = {}
-
-        def pass_out1(i, g, e):
-            cols = slice(e * P, (e + 1) * P)
+        def pass_out1(i, m, g):
             if g == 0:
-                o1_acc[i, e] = psum.tile([P, CHUNK], F32, name="acc", tag="bank", bufs=8)
+                o1_acc[i, m] = next_bank([P, BANK])
             nc.tensor.matmul_mx(
-                out=o1_acc[i, e][:],
-                lhsT=xq[:, g * 4 + i, cols].bitcast(E4X4), lhsT_scale=xs[:, g * 4 + i, cols],
-                rhs=tq[:, g * H + i // 2, :].bitcast(E5X4), rhs_scale=ts[:, g * H + i // 2, :],
+                out=o1_acc[i, m][:],
+                lhsT=x_codes[:, 2 * H * g + i, m * P : (m + 1) * P].bitcast(E4X4),
+                lhsT_scale=x_scales[:, 2 * H * g + i, m * P : (m + 1) * P],
+                rhs=t_codes[:, g * H + i // 2, :].bitcast(E5X4),
+                rhs_scale=t_scales[:, g * H + i // 2, :],
                 start=(g == 0), stop=(g == GROUPS - 1),
             )
 
-        def open_out1(i):
-            for e in range(4):
-                pass_out1(i, 0, e)
-
-        o1_sb = {}
-
-        def close_out1(i, engines, both=True):
+        def take_out1(i, m, engine):
             h, c = divmod(i, 2)
-            if c == 0:
-                o1_sb[h] = work.tile([P, 8, DH], F32, name="o1", tag="k16", bufs=6, align_bytes=256)
-            for e in range(4):
-                if both:
-                    pass_out1(i, 0, e)
-                pass_out1(i, 1, e)
-                copy_on(
-                    engines[e],
-                    out=o1_sb[h][:, 4 * c + e, :].rearrange("p (w u e) -> p w u e", u=2, e=2),
-                    in_=o1_acc[i, e][:].rearrange("p (u w e) -> p w u e", u=2, e=2),
-                )
-
-        def store_out1(i):
-            h, c = divmod(i, 2)
-            nc.sync.dma_start(
-                out=out_1[h].rearrange("(c q m) o -> c q (m o)", c=2, m=PACK)[c],
-                in_=o1_sb[h][:].rearrange("p (c m) o -> p c (m o)", c=2)[:, c, :],
+            if h not in o1_sb:
+                o1_sb[h] = placed("o1_%d" % h, [P, X_BLOCKS, DH], F32, (112, 80)[h])
+            copy_on(
+                engine,
+                out=o1_sb[h][:, 4 * c + m, :].rearrange("p (w u e) -> p w u e", u=2, e=2),
+                in_=o1_acc[i, m][:].rearrange("p (u w e) -> p w u e", u=2, e=2),
             )
 
+        def open_out1(i):
+            for m in range(4):
+                pass_out1(i, m, 0)
+
+        def close_out1(i, engines, opened=False):
+            for m in range(4):
+                if not opened:
+                    pass_out1(i, m, 0)
+                pass_out1(i, m, 1)
+                take_out1(i, m, engines[m])
+
+        def store_out1(h, lo, hi):
+            nc.sync.dma_start(out=o1_hbm[h][:, lo:hi, :], in_=o1_sb[h][:, lo:hi, :])
+
         with tc.manual_schedule():
-            load_w()
-            load_z(0, 0, 1)
+            load_w(0)
+            load_w(1)
             load_g(0)
-            load_z(0, 1, 4)
+            load_z(0, 0, 2)
+            load_z(0, 2, 4)
+            load_x(0)
             load_g(1)
             load_z(1, 0, 4)
-            load_x()
+            load_x(1)
             build_identity()
-            for c in range(2):
-                for half in range(2):
-                    sort_w(8 * c + 4 * half, 8 * c + 4 * half + 4)
+            sort_w(0, 0, 4)
+            sort_w(0, 4, 8)
             for k in range(4):
-                turn_w(0, k)
+                turn_w(0, k, "s")
+            sort_w(1, 0, 4)
+            sort_w(1, 4, 8)
+            quant_w(0)
+            for k in range(4):
+                turn_w(1, k, "sssv"[k])
+            quant_w(1)
             make_dz(0, 0, 1)
-            turn_w(1, 0)
-            turn_w(1, 1)
             turn_dz(0, 0)
-            turn_w(1, 2)
-            turn_w(1, 3)
-            quant_w(0, 0)
-            quant_w(1, 0)
-            quant_dz_feat(0, 0, 1)
             make_dz(0, 1, 2)
-            make_out0(0, 0, 0, (0,))
-            make_out0(0, 0, 1, (0,))
+            quant_f(0, 0)
             turn_dz(0, 1)
-            quant_w(0, 1)
-            quant_w(1, 1)
             make_dz(0, 2, 3)
-            make_out0(0, 0, 0, (1,))
-            make_out0(0, 0, 1, (1,))
+            out0(0, 0, 0)
+            quant_f(0, 1)
             turn_dz(0, 2)
-            quant_dz_feat(0, 1, 2)
             make_dz(0, 3, 4)
-            make_out0(0, 1, 0)
-            turn_dz(0, 3)
-            make_out0(0, 1, 1)
-            store_out0(0, 0, 2)
-            lay_dz_tok(0, 0, "v")
-            quant_dz_feat(0, 2, 3)
-            make_dz(1, 0, 1)
-            quant_dz_feat(0, 3, 4)
-            quant_dz_tok(0, 0)
-            make_dz(1, 1, 2)
-            make_out0(0, 2, 0)
-            make_out0(0, 2, 1)
-            make_out0(0, 3, 0)
-            turn_dz(1, 0)
-            turn_dz(1, 1)
-            make_dz(1, 2, 4)
-            make_out0(0, 3, 1)
-            store_out0(0, 2, 4)
-            lay_dz_tok(0, 1, "v")
-            quant_dz_feat(1, 0, 1)
-            lay_dz_tok(1, 0, "v")
-            quant_dz_tok(0, 1)
-            quant_dz_feat(1, 1, 2)
-            lay_dz_tok(1, 1, "v")
-            turn_dz(1, 2)
-            turn_dz(1, 3)
-            quant_dz_tok(1, 0)
-            quant_dz_tok(1, 1)
-            make_out0(1, 0, 0)
-            make_out0(1, 0, 1)
-            quant_dz_feat(1, 2, 4)
+            out0_bank(0, 0, 1, 0, "v")
+            out0_bank(0, 0, 1, 1)
             lay_x(0, 0, "v")
-            make_out0(1, 1, 0, (0,))
-            make_out0(1, 1, 0, (1,))
-            make_out0(1, 1, 1)
+            turn_dz(0, 3)
+            quant_f(0, 2)
+            lay_x(0, 1, "v")
+            out0(0, 1, 0)
+            out0(0, 1, 1)
+            quant_f(0, 3)
+            quant_x(0, 0)
+            lay_x(0, 2, "v")
+            quant_x(0, 1)
+            out0(0, 2, 0)
+            out0(0, 2, 1)
+            out0(0, 3, 0)
+            out0_bank(0, 3, 1, 0, "v")
+            out0_bank(0, 3, 1, 1)
+            store_out0(0, 0, 4)
+            make_dz(1, 0, 1)
+            turn_dz(1, 0)
+            make_dz(1, 1, 2)
+            turn_dz(1, 1)
+            quant_f(1, 0)
+            make_dz(1, 2, 3)
+            out0(1, 0, 0)
+            quant_f(1, 1)
+            quant_x(0, 2)
+            out0(1, 0, 1)
+            turn_dz(1, 2)
+            make_dz(1, 3, 4)
+            lay_t(0, 0)
+            out0(1, 1, 0)
+            quant_f(1, 2)
+            turn_dz(1, 3)
+            out0(1, 1, 1)
             store_out0(1, 0, 2)
+            lay_t(1, 0)
+            quant_f(1, 3)
+            quant_t(0, 0)
+            lay_x(1, 0, "v")
+            quant_t(1, 0)
+            lay_x(1, 1, "v")
+            quant_x(1, 0)
             for j in range(2, PACK):
                 for h in range(H):
-                    make_out0(1, j, h)
+                    out0(1, j, h)
             store_out0(1, 2, 4)
-            for i in range(4):
-                for g in range(GROUPS):
-                    if (g, i) != (0, 0):
-                        lay_x(g, i, "w" if (g, i) == (1, 3) else "v")
-                quant_x(0, i)
-                if i == 3:
-                    open_out1(i)
-                quant_x(1, i)
-                close_out1(i, "ssss" if i < 3 else "svsv", i < 3)
-                store_out1(i)
-                if i == 0:
-                    lay_x(1, 3, "s")
+            open_out1(0)
+            lay_x(0, 3, "s", 0, P // 2)
+            lay_t(0, 1)
+            quant_x(1, 1)
+            close_out1(0, "ssss", True)
+            store_out1(0, 0, 4)
+            open_out1(1)
+            lay_t(1, 1)
+            quant_t(0, 1)
+            lay_x(1, 2, "v")
+            quant_t(1, 1)
+            close_out1(1, "ssss", True)
+            store_out1(0, 4, 8)
+            open_out1(2)
+            lay_x(1, 3, "s", 0, P // 2)
+            lay_x(0, 3, "v", P // 2, P)
+            quant_x(1, 2)
+            quant_x(0, 3)
+            lay_x(1, 3, "v", P // 2, P)
+            quant_x(1, 3)
+            close_out1(2, "ssvs", True)
+            store_out1(1, 0, 4)
+            open_out1(3)
+            close_out1(3, "vsvs", True)
+            store_out1(1, 4, 8)

@@ -331,11 +331,13 @@ def tile_implicitrelationencoder_pb_v_kernel(
             store_out0(1, 2, 4)
             open_out1(0)
             lay_x(0, 3, "s", 0, P // 2)
-            lay_t(0, 1)
+            lay_x(0, 3, "v", P // 2, P)
             quant_x(1, 1)
             close_out1(0, "ssss", True)
             store_out1(0, 0, 4)
             open_out1(1)
+            lay_t(0, 1)
+            quant_x(0, 3)
             lay_t(1, 1)
             quant_t(0, 1)
             lay_x(1, 2, "v")
@@ -343,14 +345,12 @@ def tile_implicitrelationencoder_pb_v_kernel(
             close_out1(1, "ssss", True)
             store_out1(0, 4, 8)
             open_out1(2)
+            open_out1(3)
             lay_x(1, 3, "s", 0, P // 2)
-            lay_x(0, 3, "v", P // 2, P)
             quant_x(1, 2)
-            quant_x(0, 3)
             lay_x(1, 3, "v", P // 2, P)
             quant_x(1, 3)
             close_out1(2, "ssvs", True)
             store_out1(1, 0, 4)
-            open_out1(3)
             close_out1(3, "vsvs", True)
             store_out1(1, 4, 8)

from contextlib import ExitStack

import concourse.mybir as mybir

T, H, D, DH = 1024, 2, 1024, 512
FLOPS = 4 * T * H * D * DH
BYTES = 2 * T * H * D + 2 * H * D * DH + 4 * T * H * DH + 2 * T * H * DH + 4 * T * H * D + 4 * H * D * DH

P = 128
PACK = 4
GROUP = P * PACK
GROUPS = T // GROUP
BANK = 512
W_ROWS = 8
X_BLOCKS = D // P
KIB = 1024
LAID = {"v": 3, "s": 2}

F32 = mybir.dt.float32
BF16 = mybir.dt.bfloat16
U32 = mybir.dt.uint32
U8 = mybir.dt.uint8
E4X4 = mybir.dt.float8_e4m3fn_x4
E5X4 = mybir.dt.float8_e5m2_x4
GT = mybir.AluOpType.is_gt
MULT = mybir.AluOpType.mult
ADD = mybir.AluOpType.add
EQ = mybir.AluOpType.is_equal


def tile_implicitrelationencoder_pb_v_kernel(
    tc, out_t, out_w, out_b, self_feat, vis, z, grad_out, out_0, out_1
):
    nc = tc.nc

    def by_group(rows):
        return rows.rearrange("(g p j) d -> g p j d", g=GROUPS, j=PACK)

    x_hbm = by_group(out_t.rearrange("b n h d -> (b n) (h d)"))
    z_hbm = by_group(z.rearrange("b n d -> (b n) d"))
    g_hbm = by_group(grad_out.rearrange("b n d -> (b n) d"))
    o0_hbm = by_group(out_0.rearrange("b n h d -> (b n) (h d)"))
    w_hbm = out_w.rearrange("h (q c m) o -> c (h q) (m o)", c=2, m=W_ROWS)
    o1_hbm = out_1.rearrange("h (q m) o -> h q m o", m=X_BLOCKS)

    with ExitStack() as ctx:
        keep = ctx.enter_context(tc.tile_pool(name="keep", bufs=1))
        arena = ctx.enter_context(tc.tile_pool(name="arena", bufs=1))
        psum = ctx.enter_context(tc.psum_pool(name="psum", bufs=1))

        def placed(name, shape, dtype, at):
            return arena.tile(shape, dtype, name=name, offset=at * KIB, align_bytes=256)

        def next_bank(shape):
            return psum.tile(shape, F32, name="bank", tag="bank", bufs=8)

        def copy_on(engine, out, in_):
            if engine == "v":
                nc.vector.tensor_copy(out=out, in_=in_)
            else:
                nc.scalar.copy(out=out, in_=in_)

        def operand(name, rows, cols):
            codes = keep.tile([P, rows, cols], U32, name=name + "_codes", align_bytes=64)
            scales = keep.tile([P, rows, cols], U8, name=name + "_scales", align_bytes=64)
            return codes, scales

        w_codes, w_scales = operand("w", 2, H * BANK)
        f_codes, f_scales = operand("f", GROUPS * PACK, H * P)
        t_codes, t_scales = operand("t", GROUPS * H, DH)
        x_codes, x_scales = operand("x", GROUPS * 2 * H, BANK)
        dz = [keep.tile([P, PACK * H * DH], BF16, name="dz%d" % g, align_bytes=64) for g in range(GROUPS)]
        ident = keep.tile([P, P], F32, name="ident")

        def build_identity():
            ones = keep.tile([P, 32], F32, name="ones", align_bytes=64)
            col = keep.tile([P, 32], F32, name="col", align_bytes=64)
            row = keep.tile([P, 32], F32, name="row", align_bytes=64)
            nc.vector.memset(ones[:], 1.0)
            nc.vector.memset(ident[:], 0.0)
            nc.vector.tensor_tensor_scan(out=col[:], data0=ones[:], data1=ones[:], initial=0.0, op0=MULT, op1=ADD)
            nc.vector.transpose(out=row[:], in_=col[:])
            for q in range(0, P, 32):
                nc.vector.tensor_tensor(
                    out=ident[q : q + 32, q : q + 32], in0=col[q : q + 32, :], in1=row[q : q + 32, :], op=EQ
                )

        w_raw, w_sorted, w_turned, x_sb, z_sb, g_sb = {}, {}, {}, {}, {}, {}

        def load_w(c):
            w_raw[c] = placed("w_raw%d" % c, [P, W_ROWS * DH], BF16, 8 * c)
            nc.sync.dma_start(out=w_raw[c][:], in_=w_hbm[c])

        def load_x(g):
            x_sb[g] = placed("x%d" % g, [P, PACK, H * D], BF16, 64 + 32 * g)
            nc.sync.dma_start(out=x_sb[g][:], in_=x_hbm[g])

        def load_g(g):
            g_sb[g] = placed("g%d" % g, [P, PACK, H * DH], BF16, 112 + 8 * g)
            nc.sync.dma_start(out=g_sb[g][:], in_=g_hbm[g])

        def load_z(g, lo, hi):
            rows = placed("z%d_%d" % (g, lo), [P, hi - lo, H * DH], F32, 48 + 32 * g + 4 * lo)
            nc.sync.dma_start(out=rows[:], in_=z_hbm[g][:, lo:hi, :])
            for j in range(lo, hi):
                z_sb[g, j] = (rows, lo)

        def sort_w(c, lo, hi):
            if lo == 0:
                w_sorted[c] = placed("w_sorted%d" % c, [P, W_ROWS * DH], BF16, 16 + 8 * c)
            nc.vector.tensor_copy(
                out=w_sorted[c][:].rearrange("p (m u w e) -> p m u w e", m=W_ROWS, u=2, e=2)[:, lo:hi],
                in_=w_raw[c][:].rearrange("p (m w u e) -> p m u w e", m=W_ROWS, u=2, e=2)[:, lo:hi],
            )

        def turn_w(c, k, engine):
            if k == 0:
                w_turned[c] = placed("w_turned%d" % c, [P, P * W_ROWS * PACK], BF16, 32 + 8 * c)
            words = w_sorted[c][:].bitcast(F32)
            bank = next_bank([P, 4, P])
            for n in range(4):
                nc.tensor.transpose(bank[:, n, :], words[:, (4 * k + n) * P : (4 * k + n + 1) * P], ident[:])
            dst = w_turned[c][:].bitcast(F32).rearrange("p (h k q n) -> p k h q n", h=H, k=4, n=4)
            copy_on(engine, out=dst[:, k], in_=bank[:].rearrange("p n (h q) -> p h q n", h=H))

        def quant_w(c):
            nc.vector.quantize_mx(out=w_codes[:, c, :].bitcast(E4X4), scales=w_scales[:, c, :], in_=w_turned[c][:])

        def make_dz(g, lo, hi):
            rows, first = z_sb[g, lo]
            dst = dz[g][:].rearrange("p (j h u w e) -> p u j h w e", j=PACK, h=H, u=2, e=2)[:, :, lo:hi]
            pre = rows[:, lo - first : hi - first, :].rearrange("p j (h w u e) -> p u j h w e", h=H, u=2, e=2)
            grad = g_sb[g][:, lo:hi, :].rearrange("p j (h w u e) -> p u j h w e", h=H, u=2, e=2)
            for u in range(2):
                nc.vector.scalar_tensor_tensor(
                    out=dst[:, u], in0=pre[:, u], scalar=0.0, in1=grad[:, u], op0=GT, op1=MULT
                )

        dz_turned = {}

        def turn_dz(g, j, engine="s"):
            dz_turned[g, j] = keep.tile([P, H * P * PACK], BF16, name="dz_turned", tag="dz_turned", bufs=4, align_bytes=64)
            words = dz[g][:].bitcast(F32)
            bank = next_bank([P, 4, P])
            for n in range(4):
                nc.tensor.transpose(bank[:, n, :], words[:, (4 * j + n) * P : (4 * j + n + 1) * P], ident[:])
            copy_on(
                engine,
                out=dz_turned[g, j][:].bitcast(F32).rearrange("p (h r u) -> p h r u", h=H, u=2),
                in_=bank[:].rearrange("p (h u) r -> p h r u", u=2),
            )

        def quant_f(g, j):
            row = PACK * g + j
            nc.vector.quantize_mx(out=f_codes[:, row, :].bitcast(E5X4), scales=f_scales[:, row, :], in_=dz_turned[g, j][:])

        def laid_tile(engine):
            return keep.tile([P, BANK * PACK], BF16, name="laid", tag="laid_" + engine, bufs=LAID[engine], align_bytes=64)

        t_laid, x_laid = {}, {}

        def lay_t(g, h):
            t_laid[g, h] = laid_tile("v")
            nc.vector.tensor_copy(
                out=t_laid[g, h][:].rearrange("p (c i j) -> p c j i", i=4, j=PACK),
                in_=dz[g][:].rearrange("p (j h c i) -> p h c j i", j=PACK, h=H, i=4)[:, h],
            )

        def quant_t(g, h):
            row = g * H + h
            nc.vector.quantize_mx(out=t_codes[:, row, :].bitcast(E5X4), scales=t_scales[:, row, :], in_=t_laid[g, h][:])

        def lay_x(g, i, engine, lo=0, hi=P):
            h, c = divmod(i, 2)
            if lo == 0:
                x_laid[g, i] = laid_tile(engine)
            src = x_sb[g][:, :, h * D : (h + 1) * D].rearrange("p j (q c m) -> p c q j m", c=2, m=4)[:, c]
            dst = x_laid[g, i][:].rearrange("p (m q j) -> p q j m", m=4, j=PACK)
            copy_on(engine, out=dst[:, lo:hi], in_=src[:, lo:hi])

        def quant_x(g, i):
            row = 2 * H * g + i
            nc.vector.quantize_mx(out=x_codes[:, row, :].bitcast(E4X4), scales=x_scales[:, row, :], in_=x_laid[g, i][:])

        o0_sb, o1_sb, o0_acc, o1_acc = {}, {}, {}, {}

        def mul_out0(g, j, h, c):
            o0_acc[g, j, h, c] = next_bank([P, BANK])
            nc.tensor.matmul_mx(
                out=o0_acc[g, j, h, c][:],
                lhsT=f_codes[:, PACK * g + j, h * P : (h + 1) * P].bitcast(E5X4),
                lhsT_scale=f_scales[:, PACK * g + j, h * P : (h + 1) * P],
                rhs=w_codes[:, c, h * BANK : (h + 1) * BANK].bitcast(E4X4),
                rhs_scale=w_scales[:, c, h * BANK : (h + 1) * BANK],
                start=True, stop=True,
            )

        def take_out0(g, j, h, c, engine):
            if g not in o0_sb:
                o0_sb[g] = placed("o0_%d" % g, [P, PACK, H * D], F32, 32 * g)
            copy_on(
                engine,
                out=o0_sb[g][:, j, h * D : (h + 1) * D].rearrange("p (q c k s) -> p c q k s", c=2, k=4, s=2)[:, c],
                in_=o0_acc[g, j, h, c][:].rearrange("p (k q s) -> p q k s", k=4, s=2),
            )

        def out0_bank(g, j, h, c, engine="s"):
            mul_out0(g, j, h, c)
            take_out0(g, j, h, c, engine)

        def out0(g, j, h, engine="s"):
            for c in range(2):
                out0_bank(g, j, h, c, engine)

        def store_out0(g, lo, hi):
            nc.sync.dma_start(out=o0_hbm[g][:, lo:hi, :], in_=o0_sb[g][:, lo:hi, :])

        def pass_out1(i, m, g):
            if g == 0:
                o1_acc[i, m] = next_bank([P, BANK])
            nc.tensor.matmul_mx(
                out=o1_acc[i, m][:],
                lhsT=x_codes[:, 2 * H * g + i, m * P : (m + 1) * P].bitcast(E4X4),
                lhsT_scale=x_scales[:, 2 * H * g + i, m * P : (m + 1) * P],
                rhs=t_codes[:, g * H + i // 2, :].bitcast(E5X4),
                rhs_scale=t_scales[:, g * H + i // 2, :],
                start=(g == 0), stop=(g == GROUPS - 1),
            )

        def take_out1(i, m, engine):
            h, c = divmod(i, 2)
            if h not in o1_sb:
                o1_sb[h] = placed("o1_%d" % h, [P, X_BLOCKS, DH], F32, (112, 80)[h])
            copy_on(
                engine,
                out=o1_sb[h][:, 4 * c + m, :].rearrange("p (w u e) -> p w u e", u=2, e=2),
                in_=o1_acc[i, m][:].rearrange("p (u w e) -> p w u e", u=2, e=2),
            )

        def open_out1(i):
            for m in range(4):
                pass_out1(i, m, 0)

        def close_out1(i, engines, opened=False):
            for m in range(4):
                if not opened:
                    pass_out1(i, m, 0)
                pass_out1(i, m, 1)
                take_out1(i, m, engines[m])

        def store_out1(h, lo, hi):
            nc.sync.dma_start(out=o1_hbm[h][:, lo:hi, :], in_=o1_sb[h][:, lo:hi, :])

        with tc.manual_schedule():
            load_w(0)
            load_w(1)
            load_g(0)
            load_z(0, 0, 2)
            load_z(0, 2, 4)
            load_x(0)
            load_g(1)
            load_z(1, 0, 4)
            load_x(1)
            build_identity()
            sort_w(0, 0, 4)
            sort_w(0, 4, 8)
            for k in range(4):
                turn_w(0, k, "s")
            sort_w(1, 0, 4)
            sort_w(1, 4, 8)
            quant_w(0)
            for k in range(4):
                turn_w(1, k, "sssv"[k])
            quant_w(1)
            make_dz(0, 0, 1)
            turn_dz(0, 0)
            make_dz(0, 1, 2)
            quant_f(0, 0)
            turn_dz(0, 1)
            make_dz(0, 2, 3)
            out0(0, 0, 0)
            quant_f(0, 1)
            turn_dz(0, 2)
            make_dz(0, 3, 4)
            out0_bank(0, 0, 1, 0, "v")
            out0_bank(0, 0, 1, 1)
            lay_x(0, 0, "v")
            turn_dz(0, 3)
            quant_f(0, 2)
            lay_x(0, 1, "v")
            out0(0, 1, 0)
            out0(0, 1, 1)
            quant_f(0, 3)
            quant_x(0, 0)
            lay_x(0, 2, "v")
            quant_x(0, 1)
            out0(0, 2, 0)
            out0(0, 2, 1)
            out0(0, 3, 0)
            out0_bank(0, 3, 1, 0, "v")
            out0_bank(0, 3, 1, 1)
            store_out0(0, 0, 4)
            make_dz(1, 0, 1)
            turn_dz(1, 0)
            make_dz(1, 1, 2)
            turn_dz(1, 1)
            quant_f(1, 0)
            make_dz(1, 2, 3)
            out0(1, 0, 0)
            quant_f(1, 1)
            quant_x(0, 2)
            out0(1, 0, 1)
            turn_dz(1, 2)
            make_dz(1, 3, 4)
            lay_t(0, 0)
            out0(1, 1, 0)
            quant_f(1, 2)
            turn_dz(1, 3)
            out0(1, 1, 1)
            store_out0(1, 0, 2)
            lay_t(1, 0)
            quant_f(1, 3)
            quant_t(0, 0)
            lay_x(1, 0, "v")
            quant_t(1, 0)
            lay_x(1, 1, "v")
            quant_x(1, 0)
            for j in range(2, PACK):
                for h in range(H):
                    out0(1, j, h)
            store_out0(1, 2, 4)
            open_out1(0)
            lay_x(0, 3, "s", 0, P // 2)
            lay_x(0, 3, "v", P // 2, P)
            quant_x(1, 1)
            close_out1(0, "ssss", True)
            store_out1(0, 0, 4)
            open_out1(1)
            lay_t(0, 1)
            quant_x(0, 3)
            lay_t(1, 1)
            quant_t(0, 1)
            lay_x(1, 2, "v")
            quant_t(1, 1)
            close_out1(1, "ssss", True)
            store_out1(0, 4, 8)
            open_out1(2)
            open_out1(3)
            lay_x(1, 3, "s", 0, P // 2)
            quant_x(1, 2)
            lay_x(1, 3, "v", P // 2, P)
            quant_x(1, 3)
            close_out1(2, "ssvs", True)
            store_out1(1, 0, 4)
            close_out1(3, "vsvs", True)
            store_out1(1, 4, 8)
